import numpy as np
import ml_dtypes


def mxq(x, axis, fmt="e4m3"):
    dtype, down = {"e4m3": (ml_dtypes.float8_e4m3fn, 7), "e5m2": (ml_dtypes.float8_e5m2, 14)}[fmt]
    v = np.moveaxis(np.asarray(x, np.float32).astype(ml_dtypes.bfloat16).astype(np.float64), axis, -1)
    blocks = v.reshape(v.shape[:-1] + (-1, 32))
    amax = np.abs(blocks).max(-1, keepdims=True)
    byte = np.maximum(np.where(amax > 0, np.frexp(amax)[1] - 1 + 127, 0) - down, 1)
    scale = np.exp2(byte - 127.0)
    codes = (blocks / scale).astype(np.float32).astype(dtype).astype(np.float64)
    return np.moveaxis((codes * scale).reshape(v.shape), -1, axis)


WIDE = False


def mx_kscale(k):
    if not WIDE:
        return np.ones(k)
    levels = np.array([10, -10, 5, -5, 0])
    a = np.random.permutation(np.resize(levels, k // 512 * 4)).reshape(k // 512, 4)
    idx = np.arange(k)
    return np.exp2(a[idx // 512, idx % 128 // 32])


BF16 = ml_dtypes.bfloat16


def bf(x):
    return np.asarray(x, np.float32).astype(BF16)


def f64(x):
    return np.asarray(x).astype(np.float64)


B, C, T, TF, CCONF, GROUPS = 8, 512, 64, 256, 14336, 32
EPS = 1e-5
KP = 4 * C + CCONF


def group_norm(x, gamma, beta):
    b_, c_, t_ = x.shape
    xg = x.reshape(b_, GROUPS, c_ // GROUPS, t_)
    mu = xg.mean(axis=(2, 3), keepdims=True)
    var = xg.var(axis=(2, 3), keepdims=True)
    xg = (xg - mu) / np.sqrt(var + EPS)
    return xg.reshape(b_, c_, t_) * gamma[None, :, None] + beta[None, :, None]


def setup_inputs():
    s, u = mx_kscale(C), mx_kscale(KP)
    u_roi, u_prop, u_cur, u_conf = u[:C], u[C:3 * C], u[3 * C:4 * C], u[4 * C:]
    return {
        'feature': bf(np.random.standard_normal((B, C, T)) * s[None, :, None]),
        'prop_roi': bf(np.maximum(np.random.standard_normal((B, C, T)), 0.0) * u_roi[None, :, None]),
        'prop_feature': bf(np.abs(np.random.standard_normal((B, 2 * C, T))) * 1.5 * u_prop[None, :, None]),
        'conf_result_feature': bf(np.random.standard_normal((B, CCONF, T)) * u_conf[None, :, None]),
        'w_cur': bf(np.random.standard_normal((C, C)) * C ** -0.5 / s[None, :]),
        'b_cur': bf(np.random.standard_normal(C) * 0.3),
        'g_cur': bf((1.0 + 0.2 * np.random.standard_normal(C)) * u_cur),
        'be_cur': bf(np.random.standard_normal(C) * 0.3 * u_cur),
        'w_prop': bf(np.random.standard_normal((C, KP)) * KP ** -0.5 / u[None, :]),
        'b_prop': bf(np.random.standard_normal(C) * 0.3),
        'g_prop': bf(1.0 + 0.2 * np.random.standard_normal(C)),
        'be_prop': bf(np.random.standard_normal(C) * 0.3),
    }


def reference(feature, prop_roi, prop_feature, conf_result_feature, w_cur, b_cur, g_cur, be_cur, w_prop, b_prop, g_prop, be_prop):
    y = (mxq(f64(w_cur), 1, 'e4m3') @ mxq(f64(feature), 1, 'e4m3')) + f64(b_cur)[None, :, None]
    fm_short = np.maximum(group_norm(y, f64(g_cur), f64(be_cur)), 0.0)
    cat = np.concatenate([f64(prop_roi), f64(prop_feature), fm_short, f64(conf_result_feature)], axis=1)
    z = (mxq(f64(w_prop), 1, 'e4m3') @ mxq(cat, 1, 'e4m3')) + f64(b_prop)[None, :, None]
    return np.maximum(group_norm(z, f64(g_prop), f64(be_prop)), 0.0)

@@ -1,0 +1,292 @@
+from contextlib import ExitStack
+
+import concourse.mybir as mybir
+from concourse.masks import make_identity
+
+BF16 = mybir.dt.bfloat16
+F32 = mybir.dt.float32
+U32 = mybir.dt.uint32
+U8 = mybir.dt.uint8
+FP8X4 = mybir.dt.float8_e4m3fn_x4
+ACT = mybir.ActivationFunctionType
+ALU = mybir.AluOpType
+AX = mybir.AxisListType
+
+P = 128
+PACK = 4
+K_PASS = P * PACK
+BATCH = 8
+TIMES = 64
+COLS = BATCH * TIMES
+CHANNELS = 512
+K_CAT = 16384
+PASSES = K_CAT // K_PASS
+FM_PASS = 3
+GROUP_VALUES = 16 * TIMES
+EPS = 1e-5
+
+CHUNK_PASSES = 4
+CHUNK_K = CHUNK_PASSES * K_PASS
+CHUNKS = PASSES // CHUNK_PASSES
+RUN_PASSES = 2
+
+FLOPS = 2 * COLS * CHANNELS * (CHANNELS + K_CAT)
+
+
+def load_stream_pass(nc, raw, stream, first_channel):
+    channels = stream[:, first_channel : first_channel + K_PASS, :]
+    nc.sync.dma_start(
+        out=raw[:].rearrange("p b i t -> p b (i t)"),
+        in_=channels.rearrange("b (p i) t -> p b (i t)", i=PACK),
+    )
+
+
+def group_stream_words(nc, grouped, raw):
+    nc.vector.tensor_copy(
+        out=grouped[:].rearrange("p (b c r i) -> p b c i r", b=BATCH, r=4, i=PACK),
+        in_=raw[:].rearrange("p b i (c r) -> p b c i r", r=4),
+    )
+
+
+def transpose_weights(nc, psum, grouped, words, first_word, ident):
+    grouped_words = grouped[:].bitcast(F32).rearrange("q (c u) -> q c u", u=2)
+    for half in range(2):
+        planes = psum.tile([P, 2, 2 * P], F32, tag="bank", name="planes")
+        for u in range(2):
+            for i in range(2):
+                nc.tensor.transpose(
+                    planes[:, u, i * P : (i + 1) * P],
+                    words[:, 2 * half + i, first_word + u : first_word + 2 * P : 2],
+                    ident[:],
+                )
+        nc.scalar.copy(
+            out=grouped_words[:, half * 2 * P : (half + 1) * 2 * P, :],
+            in_=planes[:].rearrange("q u c -> q c u"),
+        )
+
+
+def quantise(nc, pool, grouped, name):
+    codes = pool.tile([P, COLS], U32, align_bytes=64, name=name + "_codes")
+    scales = pool.tile([P, COLS], U8, align_bytes=64, name=name + "_scales")
+    nc.vector.quantize_mx(out=codes[:].bitcast(FP8X4), scales=scales[:], in_=grouped[:])
+    return codes, scales
+
+
+def multiply_pass(nc, sums, weights, stream, start, stop):
+    w_codes, w_scales = weights
+    s_codes, s_scales = stream
+    for j in range(PACK):
+        rows = slice(j * P, (j + 1) * P)
+        nc.tensor.matmul_mx(
+            out=sums[j][:],
+            lhsT=w_codes[:, rows].bitcast(FP8X4),
+            lhsT_scale=w_scales[:, rows],
+            rhs=s_codes[:].bitcast(FP8X4),
+            rhs_scale=s_scales[:],
+            start=start,
+            stop=stop,
+        )
+
+
+def group_norm_relu(nc, work, psum, sums, group_mean, bias, gamma, beta, result):
+    y = work.tile([P, PACK, BATCH, TIMES], F32, name="y")
+    squares = work.tile([P, PACK, BATCH, TIMES], F32, name="squares")
+    row_sums = work.tile([P, PACK, 2, BATCH], F32, name="row_sums")
+    for j in range(PACK):
+        nc.scalar.activation(
+            out=y[:, j, :, :].rearrange("p b t -> p (b t)"),
+            in_=sums[j][:],
+            func=ACT.Identity,
+            bias=bias[:, j : j + 1],
+        )
+        nc.scalar.activation(
+            out=squares[:, j, :, :].rearrange("p b t -> p (b t)"),
+            in_=sums[j][:],
+            func=ACT.Square,
+            bias=bias[:, j : j + 1],
+        )
+        nc.vector.tensor_reduce(out=row_sums[:, j, 0, :], in_=y[:, j, :, :], axis=AX.X, op=ALU.add)
+        nc.vector.tensor_reduce(out=row_sums[:, j, 1, :], in_=squares[:, j, :, :], axis=AX.X, op=ALU.add)
+
+    moments_psum = psum.tile([P, 2, BATCH], F32, tag="bank", name="moments_psum")
+    for j in range(PACK):
+        nc.tensor.matmul(
+            out=moments_psum[:].rearrange("p s b -> p (s b)"),
+            lhsT=group_mean[:].rearrange("p g r -> p (g r)"),
+            rhs=row_sums[:, j, :, :].rearrange("p s b -> p (s b)"),
+            start=(j == 0),
+            stop=(j == PACK - 1),
+        )
+    moments = work.tile([P, 2, BATCH], F32, name="moments")
+    nc.vector.tensor_copy(out=moments[:], in_=moments_psum[:])
+    mean = moments[:, 0, :]
+    mean_of_squares = moments[:, 1, :]
+
+    var = work.tile([P, BATCH], F32, name="var")
+    std = work.tile([P, BATCH], F32, name="std")
+    rstd = work.tile([P, BATCH], F32, name="rstd")
+    shift = work.tile([P, BATCH], F32, name="shift")
+    nc.vector.tensor_tensor(out=var[:], in0=mean, in1=mean, op=ALU.mult)
+    nc.vector.tensor_tensor(out=var[:], in0=mean_of_squares, in1=var[:], op=ALU.subtract)
+    nc.vector.tensor_scalar(out=var[:], in0=var[:], scalar1=0.0, scalar2=EPS, op0=ALU.max, op1=ALU.add)
+    nc.scalar.activation(out=std[:], in_=var[:], func=ACT.Sqrt)
+    nc.vector.reciprocal(out=rstd[:], in_=std[:])
+    nc.vector.scalar_tensor_tensor(
+        out=shift[:], in0=mean, scalar=-1.0, in1=rstd[:], op0=ALU.mult, op1=ALU.mult
+    )
+
+    for b in range(BATCH):
+        nc.vector.tensor_scalar(
+            out=y[:, :, b, :],
+            in0=y[:, :, b, :],
+            scalar1=rstd[:, b : b + 1],
+            scalar2=shift[:, b : b + 1],
+            op0=ALU.mult,
+            op1=ALU.add,
+        )
+    for j in range(PACK):
+        nc.scalar.activation(
+            out=result[:, :, j, :],
+            in_=y[:, j, :, :],
+            func=ACT.Relu,
+            bias=beta[:, j : j + 1],
+            scale=gamma[:, j : j + 1],
+        )
+
+
+def tile_coarsepyramid_pc_k_kernel(
+    tc,
+    feature,
+    prop_roi,
+    prop_feature,
+    conf_result_feature,
+    w_cur,
+    b_cur,
+    g_cur,
+    be_cur,
+    w_prop,
+    b_prop,
+    g_prop,
+    be_prop,
+    out,
+):
+    nc = tc.nc
+
+    def given_stream(g):
+        if g == 0:
+            return prop_roi, 0
+        if g < FM_PASS:
+            return prop_feature, (g - 1) * K_PASS
+        return conf_result_feature, (g - FM_PASS - 1) * K_PASS
+
+    with ExitStack() as stack:
+        const = stack.enter_context(tc.tile_pool(name="const", bufs=1))
+        work = stack.enter_context(tc.tile_pool(name="work", bufs=1))
+        w_pool = stack.enter_context(tc.tile_pool(name="w_pool", bufs=3))
+        raw_pool = stack.enter_context(tc.tile_pool(name="raw_pool", bufs=8))
+        grouped_pool = stack.enter_context(tc.tile_pool(name="grouped_pool", bufs=2 * RUN_PASSES))
+        operand_pool = stack.enter_context(tc.tile_pool(name="operand_pool", bufs=3 * RUN_PASSES))
+        sums_pool = stack.enter_context(tc.psum_pool(name="sums_pool", bufs=1))
+        bank_pool = stack.enter_context(tc.psum_pool(name="bank_pool", bufs=4))
+
+        w_cur_raw = const.tile([P, PACK, K_PASS], BF16)
+        nc.sync.dma_start(out=w_cur_raw[:], in_=w_cur.rearrange("(p j) k -> p j k", j=PACK))
+        feature_raw = raw_pool.tile([P, BATCH, PACK, TIMES], BF16, name="raw")
+        load_stream_pass(nc, feature_raw, feature, 0)
+
+        vectors_bf16 = const.tile([P, 6, 16], BF16)
+        for v, vector in enumerate((b_cur, g_cur, be_cur, b_prop, g_prop, be_prop)):
+            nc.scalar.dma_start(
+                out=vectors_bf16[:, v, 0:PACK], in_=vector.rearrange("(p j) -> p j", j=PACK)
+            )
+        vectors = const.tile([P, 6, PACK], F32)
+        nc.vector.tensor_copy(out=vectors[:], in_=vectors_bf16[:, :, 0:PACK])
+
+        one = const.tile([P, 1], F32)
+        nc.vector.memset(one[:], 1.0)
+        nc.scalar.activation(out=one[:], in_=one[:], func=ACT.Sqrt)
+
+        ident = const.tile([P, P], F32)
+        make_identity(nc, ident[:])
+        same_group = const.tile([P, P // PACK], F32)
+        nc.vector.tensor_reduce(
+            out=same_group[:], in_=ident[:].rearrange("p (g r) -> p g r", r=PACK), axis=AX.X, op=ALU.add
+        )
+        group_mean = const.tile([P, P // PACK, PACK], F32)
+        nc.vector.tensor_scalar(
+            out=group_mean[:],
+            in0=same_group[:].unsqueeze(2).to_broadcast([P, P // PACK, PACK]),
+            scalar1=1.0 / GROUP_VALUES,
+            scalar2=None,
+            op0=ALU.mult,
+        )
+
+        def new_sums():
+            return [sums_pool.tile([P, COLS], F32, name="sums%d" % j) for j in range(PACK)]
+
+        w_grouped = grouped_pool.tile([P, CHANNELS * PACK], BF16, align_bytes=64, name="w_grouped")
+        transpose_weights(nc, bank_pool, w_grouped, w_cur_raw[:].bitcast(F32), 0, ident)
+        s_grouped = grouped_pool.tile([P, COLS * PACK], BF16, align_bytes=64, name="s_grouped")
+        group_stream_words(nc, s_grouped, feature_raw)
+        weights = quantise(nc, operand_pool, w_grouped, "w")
+        stream = quantise(nc, operand_pool, s_grouped, "s")
+        y_sums = new_sums()
+        multiply_pass(nc, y_sums, weights, stream, True, True)
+        fm_raw = const.tile([P, BATCH, PACK, TIMES], BF16)
+        group_norm_relu(
+            nc, work, bank_pool, y_sums, group_mean,
+            vectors[:, 0, :], vectors[:, 1, :], vectors[:, 2, :], fm_raw[:],
+        )
+
+        chunk_order = [1, 0] + list(range(2, CHUNKS))
+        z_sums = new_sums()
+        waiting = []
+        multiplied = 0
+
+        for chunk in chunk_order:
+            w_raw = w_pool.tile([P, PACK, CHUNK_K], BF16, name="w_raw")
+            nc.sync.dma_start(
+                out=w_raw[:],
+                in_=w_prop[:, chunk * CHUNK_K : (chunk + 1) * CHUNK_K].rearrange("(p j) k -> p j k", j=PACK),
+            )
+            w_words = w_raw[:].bitcast(F32)
+            for first in range(0, CHUNK_PASSES, RUN_PASSES):
+                run = range(first, first + RUN_PASSES)
+                w_tiles = []
+                s_tiles = []
+                for c in run:
+                    w_grouped = grouped_pool.tile([P, CHANNELS * PACK], BF16, align_bytes=64, name="w_grouped")
+                    transpose_weights(nc, bank_pool, w_grouped, w_words, c * K_PASS // 2, ident)
+                    w_tiles.append(w_grouped)
+                for c in run:
+                    g = chunk * CHUNK_PASSES + c
+                    if g == FM_PASS:
+                        raw = fm_raw
+                    else:
+                        raw = raw_pool.tile([P, BATCH, PACK, TIMES], BF16, name="raw")
+                        source, first_channel = given_stream(g)
+                        load_stream_pass(nc, raw, source, first_channel)
+                    s_grouped = grouped_pool.tile([P, COLS * PACK], BF16, align_bytes=64, name="s_grouped")
+                    group_stream_words(nc, s_grouped, raw)
+                    s_tiles.append(s_grouped)
+                prepared = [
+                    (quantise(nc, operand_pool, w_tiles[n], "w"), quantise(nc, operand_pool, s_tiles[n], "s"))
+                    for n in range(RUN_PASSES)
+                ]
+                for weights, stream in waiting:
+                    multiply_pass(nc, z_sums, weights, stream, multiplied == 0, False)
+                    multiplied += 1
+                waiting = prepared
+        for weights, stream in waiting:
+            multiply_pass(nc, z_sums, weights, stream, False, multiplied == PASSES - 1)
+            multiplied += 1
+
+        result = work.tile([P, BATCH, PACK, TIMES], F32, name="result")
+        group_norm_relu(
+            nc, work, bank_pool, z_sums, group_mean,
+            vectors[:, 3, :], vectors[:, 4, :], vectors[:, 5, :], result[:],
+        )
+        nc.sync.dma_start(
+            out=out.rearrange("b (p j) t -> p b (j t)", j=PACK),
+            in_=result[:].rearrange("p b j t -> p b (j t)"),
+        )

@@ -27,8 +27,10 @@ EPS = 1e-5
 
 CHUNK_PASSES = 4
 CHUNK_K = CHUNK_PASSES * K_PASS
-CHUNKS = PASSES // CHUNK_PASSES
 RUN_PASSES = 2
+RUN_K = RUN_PASSES * K_PASS
+VECTOR_TIMES = 40
+CHUNK_ORDER = (1, 2, 3, 4, 0, 5, 6, 7)
 
 FLOPS = 2 * COLS * CHANNELS * (CHANNELS + K_CAT)
 
@@ -41,10 +43,18 @@ def load_stream_pass(nc, raw, stream, first_channel):
     )
 
 
-def group_stream_words(nc, grouped, raw):
+def group_on_vector(nc, grouped, raw):
+    blocks = VECTOR_TIMES // 4
     nc.vector.tensor_copy(
-        out=grouped[:].rearrange("p (b c r i) -> p b c i r", b=BATCH, r=4, i=PACK),
-        in_=raw[:].rearrange("p b i (c r) -> p b c i r", r=4),
+        out=grouped[:].rearrange("p (b c r i) -> p b c i r", b=BATCH, r=4, i=PACK)[:, :, 0:blocks, :, :],
+        in_=raw[:].rearrange("p b i (c r) -> p b c i r", r=4)[:, :, 0:blocks, :, :],
+    )
+
+
+def group_on_scalar(nc, grouped, raw):
+    nc.scalar.copy(
+        out=grouped[:].rearrange("p (b t i) -> p b t i", b=BATCH, i=PACK)[:, :, VECTOR_TIMES:TIMES, :],
+        in_=raw[:].rearrange("p b i t -> p b t i")[:, :, VECTOR_TIMES:TIMES, :],
     )
 
 
@@ -63,7 +73,6 @@ def transpose_weights(nc, psum, grouped, words, first_word, ident):
             out=grouped_words[:, half * 2 * P : (half + 1) * 2 * P, :],
             in_=planes[:].rearrange("q u c -> q c u"),
         )
-
 
 def quantise(nc, pool, grouped, name):
     codes = pool.tile([P, COLS], U32, align_bytes=64, name=name + "_codes")
@@ -88,26 +97,7 @@ def multiply_pass(nc, sums, weights, stream, start, stop):
         )
 
 
-def group_norm_relu(nc, work, psum, sums, group_mean, bias, gamma, beta, result):
-    y = work.tile([P, PACK, BATCH, TIMES], F32, name="y")
-    squares = work.tile([P, PACK, BATCH, TIMES], F32, name="squares")
-    row_sums = work.tile([P, PACK, 2, BATCH], F32, name="row_sums")
-    for j in range(PACK):
-        nc.scalar.activation(
-            out=y[:, j, :, :].rearrange("p b t -> p (b t)"),
-            in_=sums[j][:],
-            func=ACT.Identity,
-            bias=bias[:, j : j + 1],
-        )
-        nc.scalar.activation(
-            out=squares[:, j, :, :].rearrange("p b t -> p (b t)"),
-            in_=sums[j][:],
-            func=ACT.Square,
-            bias=bias[:, j : j + 1],
-        )
-        nc.vector.tensor_reduce(out=row_sums[:, j, 0, :], in_=y[:, j, :, :], axis=AX.X, op=ALU.add)
-        nc.vector.tensor_reduce(out=row_sums[:, j, 1, :], in_=squares[:, j, :, :], axis=AX.X, op=ALU.add)
-
+def group_moments(nc, psum, work, row_sums, group_mean):
     moments_psum = psum.tile([P, 2, BATCH], F32, tag="bank", name="moments_psum")
     for j in range(PACK):
         nc.tensor.matmul(
@@ -119,22 +109,26 @@ def group_norm_relu(nc, work, psum, sums, group_mean, bias, gamma, beta, result)
         )
     moments = work.tile([P, 2, BATCH], F32, name="moments")
     nc.vector.tensor_copy(out=moments[:], in_=moments_psum[:])
-    mean = moments[:, 0, :]
-    mean_of_squares = moments[:, 1, :]
-
     var = work.tile([P, BATCH], F32, name="var")
+    nc.vector.tensor_tensor(out=var[:], in0=moments[:, 0, :], in1=moments[:, 0, :], op=ALU.mult)
+    nc.vector.tensor_tensor(out=var[:], in0=moments[:, 1, :], in1=var[:], op=ALU.subtract)
+    nc.vector.tensor_scalar(out=var[:], in0=var[:], scalar1=0.0, scalar2=EPS, op0=ALU.max, op1=ALU.add)
+    return moments, var
+
+
+def square_root(nc, work, var):
     std = work.tile([P, BATCH], F32, name="std")
+    nc.scalar.activation(out=std[:], in_=var[:], func=ACT.Sqrt)
+    return std
+
+
+def normalise(nc, work, y, moments, std):
     rstd = work.tile([P, BATCH], F32, name="rstd")
     shift = work.tile([P, BATCH], F32, name="shift")
-    nc.vector.tensor_tensor(out=var[:], in0=mean, in1=mean, op=ALU.mult)
-    nc.vector.tensor_tensor(out=var[:], in0=mean_of_squares, in1=var[:], op=ALU.subtract)
-    nc.vector.tensor_scalar(out=var[:], in0=var[:], scalar1=0.0, scalar2=EPS, op0=ALU.max, op1=ALU.add)
-    nc.scalar.activation(out=std[:], in_=var[:], func=ACT.Sqrt)
     nc.vector.reciprocal(out=rstd[:], in_=std[:])
     nc.vector.scalar_tensor_tensor(
-        out=shift[:], in0=mean, scalar=-1.0, in1=rstd[:], op0=ALU.mult, op1=ALU.mult
+        out=shift[:], in0=moments[:, 0, :], scalar=-1.0, in1=rstd[:], op0=ALU.mult, op1=ALU.mult
     )
-
     for b in range(BATCH):
         nc.vector.tensor_scalar(
             out=y[:, :, b, :],
@@ -144,6 +138,9 @@ def group_norm_relu(nc, work, psum, sums, group_mean, bias, gamma, beta, result)
             op0=ALU.mult,
             op1=ALU.add,
         )
+
+
+def affine_relu(nc, y, gamma, beta, result):
     for j in range(PACK):
         nc.scalar.activation(
             out=result[:, :, j, :],
@@ -152,7 +149,6 @@ def group_norm_relu(nc, work, psum, sums, group_mean, bias, gamma, beta, result)
             bias=beta[:, j : j + 1],
             scale=gamma[:, j : j + 1],
         )
-
 
 def tile_coarsepyramid_pc_k_kernel(
     tc,
@@ -182,30 +178,17 @@ def tile_coarsepyramid_pc_k_kernel(
     with ExitStack() as stack:
         const = stack.enter_context(tc.tile_pool(name="const", bufs=1))
         work = stack.enter_context(tc.tile_pool(name="work", bufs=1))
+        first_pool = stack.enter_context(tc.tile_pool(name="first_pool", bufs=2))
         w_pool = stack.enter_context(tc.tile_pool(name="w_pool", bufs=3))
-        raw_pool = stack.enter_context(tc.tile_pool(name="raw_pool", bufs=8))
+        raw_pool = stack.enter_context(tc.tile_pool(name="raw_pool", bufs=10))
         grouped_pool = stack.enter_context(tc.tile_pool(name="grouped_pool", bufs=2 * RUN_PASSES))
         operand_pool = stack.enter_context(tc.tile_pool(name="operand_pool", bufs=3 * RUN_PASSES))
         sums_pool = stack.enter_context(tc.psum_pool(name="sums_pool", bufs=1))
         bank_pool = stack.enter_context(tc.psum_pool(name="bank_pool", bufs=4))
 
-        w_cur_raw = const.tile([P, PACK, K_PASS], BF16)
-        nc.sync.dma_start(out=w_cur_raw[:], in_=w_cur.rearrange("(p j) k -> p j k", j=PACK))
-        feature_raw = raw_pool.tile([P, BATCH, PACK, TIMES], BF16, name="raw")
-        load_stream_pass(nc, feature_raw, feature, 0)
-
-        vectors_bf16 = const.tile([P, 6, 16], BF16)
-        for v, vector in enumerate((b_cur, g_cur, be_cur, b_prop, g_prop, be_prop)):
-            nc.scalar.dma_start(
-                out=vectors_bf16[:, v, 0:PACK], in_=vector.rearrange("(p j) -> p j", j=PACK)
-            )
-        vectors = const.tile([P, 6, PACK], F32)
-        nc.vector.tensor_copy(out=vectors[:], in_=vectors_bf16[:, :, 0:PACK])
-
         one = const.tile([P, 1], F32)
         nc.vector.memset(one[:], 1.0)
         nc.scalar.activation(out=one[:], in_=one[:], func=ACT.Sqrt)
-
         ident = const.tile([P, P], F32)
         make_identity(nc, ident[:])
         same_group = const.tile([P, P // PACK], F32)
@@ -221,72 +204,160 @@ def tile_coarsepyramid_pc_k_kernel(
             op0=ALU.mult,
         )
 
+        runs = [[-1]]
+        for chunk in CHUNK_ORDER:
+            for first in range(0, CHUNK_PASSES, RUN_PASSES):
+                runs.append([chunk * CHUNK_PASSES + first + n for n in range(RUN_PASSES)])
+        w_words = {}
+        raws = {}
+        w_cur_raw = const.tile([P, PACK, K_PASS], BF16)
+        fm_raw = const.tile([P, BATCH, PACK, TIMES], BF16)
+
+        def load_weights(passes, tile):
+            k0 = passes[0] * K_PASS
+            nc.sync.dma_start(
+                out=tile[:],
+                in_=w_prop[:, k0 : k0 + len(passes) * K_PASS].rearrange("(p j) k -> p j k", j=PACK),
+            )
+            words = tile[:].bitcast(F32)
+            for n, g in enumerate(passes):
+                w_words[g] = (words, n * K_PASS // 2)
+
+        def load_run(s):
+            if s >= len(runs):
+                return
+            if s == 0:
+                nc.sync.dma_start(out=w_cur_raw[:], in_=w_cur.rearrange("(p j) k -> p j k", j=PACK))
+                w_words[-1] = (w_cur_raw[:].bitcast(F32), 0)
+            elif s <= 2:
+                w_half = first_pool.tile([P, PACK, RUN_K], BF16, name="w_half")
+                load_weights(runs[s], w_half)
+            elif s % 2 == 1:
+                w_raw = w_pool.tile([P, PACK, CHUNK_K], BF16, name="w_raw")
+                load_weights(runs[s] + runs[s + 1], w_raw)
+            for g in runs[s]:
+                if g == FM_PASS:
+                    raws[g] = fm_raw
+                    continue
+                raw = raw_pool.tile([P, BATCH, PACK, TIMES], BF16, name="raw")
+                if g < 0:
+                    load_stream_pass(nc, raw, feature, 0)
+                else:
+                    source, first_channel = given_stream(g)
+                    load_stream_pass(nc, raw, source, first_channel)
+                raws[g] = raw
+
+        PREFETCH = 4
+        for s in range(PREFETCH):
+            load_run(s)
+
+        vectors_bf16 = const.tile([P, 6, 16], BF16)
+        for v, vector in enumerate((b_cur, g_cur, be_cur, b_prop, g_prop, be_prop)):
+            nc.scalar.dma_start(
+                out=vectors_bf16[:, v, 0:PACK], in_=vector.rearrange("(p j) -> p j", j=PACK)
+            )
+        vectors = const.tile([P, 6, PACK], F32)
+        nc.vector.tensor_copy(out=vectors[:], in_=vectors_bf16[:, :, 0:PACK])
+
+        s_grouped = {}
+        w_grouped = {}
+        operands = {}
+
+        def regroup(s):
+            if s >= len(runs):
+                return
+            for g in runs[s]:
+                grouped = grouped_pool.tile([P, COLS * PACK], BF16, align_bytes=64, name="s_grouped")
+                group_on_vector(nc, grouped, raws[g])
+                group_on_scalar(nc, grouped, raws[g])
+                s_grouped[g] = grouped
+
+        def transpose_run(s):
+            for g in runs[s]:
+                grouped = grouped_pool.tile([P, CHANNELS * PACK], BF16, align_bytes=64, name="w_grouped")
+                words, first_word = w_words[g]
+                transpose_weights(nc, bank_pool, grouped, words, first_word, ident)
+                w_grouped[g] = grouped
+
+        def quantise_run(s):
+            for g in runs[s]:
+                operands[g] = [None, quantise(nc, operand_pool, s_grouped[g], "s")]
+            for g in runs[s]:
+                operands[g][0] = quantise(nc, operand_pool, w_grouped[g], "w")
+
         def new_sums():
             return [sums_pool.tile([P, COLS], F32, name="sums%d" % j) for j in range(PACK)]
 
-        w_grouped = grouped_pool.tile([P, CHANNELS * PACK], BF16, align_bytes=64, name="w_grouped")
-        transpose_weights(nc, bank_pool, w_grouped, w_cur_raw[:].bitcast(F32), 0, ident)
-        s_grouped = grouped_pool.tile([P, COLS * PACK], BF16, align_bytes=64, name="s_grouped")
-        group_stream_words(nc, s_grouped, feature_raw)
-        weights = quantise(nc, operand_pool, w_grouped, "w")
-        stream = quantise(nc, operand_pool, s_grouped, "s")
-        y_sums = new_sums()
-        multiply_pass(nc, y_sums, weights, stream, True, True)
-        fm_raw = const.tile([P, BATCH, PACK, TIMES], BF16)
-        group_norm_relu(
-            nc, work, bank_pool, y_sums, group_mean,
-            vectors[:, 0, :], vectors[:, 1, :], vectors[:, 2, :], fm_raw[:],
-        )
+        y = work.tile([P, PACK, BATCH, TIMES], F32, name="y")
+        squares = work.tile([P, PACK, BATCH, TIMES], F32, name="squares")
+        row_sums = work.tile([P, PACK, 2, BATCH], F32, name="row_sums")
 
-        chunk_order = [1, 0] + list(range(2, CHUNKS))
-        z_sums = new_sums()
-        waiting = []
-        multiplied = 0
+        def flat(tile, j):
+            return tile[:, j, :, :].rearrange("p b t -> p (b t)")
 
-        for chunk in chunk_order:
-            w_raw = w_pool.tile([P, PACK, CHUNK_K], BF16, name="w_raw")
+        def reduce_rows(source, j, s):
+            nc.vector.tensor_reduce(out=row_sums[:, j, s, :], in_=source[:, j, :, :], axis=AX.X, op=ALU.add)
+
+        with tc.manual_schedule():
+            sums = new_sums()
+            multiplied = 0
+            regroup(0)
+            for s in range(len(runs) + 1):
+                load_run(s + PREFETCH)
+                if s == 2:
+                    for j in range(2):
+                        nc.scalar.activation(
+                            out=flat(y, j), in_=sums[j][:], func=ACT.Identity, bias=vectors[:, 0, j : j + 1]
+                        )
+                    for j in range(2, PACK):
+                        nc.vector.tensor_scalar(
+                            out=flat(y, j), in0=sums[j][:], scalar1=vectors[:, 0, j : j + 1], scalar2=None, op0=ALU.add
+                        )
+                    sums = new_sums()
+                if s == 7:
+                    moments, var = group_moments(nc, bank_pool, work, row_sums, group_mean)
+                if s < len(runs):
+                    transpose_run(s)
+                if s == 7:
+                    std = square_root(nc, work, var)
+                if s >= 1:
+                    for g in runs[s - 1]:
+                        weights, stream = operands[g][0], operands[g][1]
+                        if g < 0:
+                            multiply_pass(nc, sums, weights, stream, True, True)
+                        else:
+                            multiply_pass(nc, sums, weights, stream, multiplied == 0, multiplied == PASSES - 1)
+                            multiplied += 1
+                if s in (3, 4):
+                    for j in (2 * s - 6, 2 * s - 5):
+                        reduce_rows(y, j, 0)
+                        nc.scalar.activation(out=flat(squares, j), in_=flat(y, j), func=ACT.Square)
+                if s in (5, 6):
+                    for j in (2 * s - 10, 2 * s - 9):
+                        reduce_rows(squares, j, 1)
+                if s == 8:
+                    normalise(nc, work, y, moments, std)
+                regroup(s + 1)
+                if s == 8:
+                    affine_relu(nc, y, vectors[:, 1, :], vectors[:, 2, :], fm_raw)
+                if s < len(runs):
+                    quantise_run(s)
+
+            for j in range(PACK):
+                nc.scalar.activation(
+                    out=flat(y, j), in_=sums[j][:], func=ACT.Identity, bias=vectors[:, 3, j : j + 1]
+                )
+                nc.scalar.activation(
+                    out=flat(squares, j), in_=sums[j][:], func=ACT.Square, bias=vectors[:, 3, j : j + 1]
+                )
+                reduce_rows(y, j, 0)
+                reduce_rows(squares, j, 1)
+            moments, var = group_moments(nc, bank_pool, work, row_sums, group_mean)
+            std = square_root(nc, work, var)
+            normalise(nc, work, y, moments, std)
+            result = work.tile([P, BATCH, PACK, TIMES], F32, name="result")
+            affine_relu(nc, y, vectors[:, 4, :], vectors[:, 5, :], result)
             nc.sync.dma_start(
-                out=w_raw[:],
-                in_=w_prop[:, chunk * CHUNK_K : (chunk + 1) * CHUNK_K].rearrange("(p j) k -> p j k", j=PACK),
+                out=out.rearrange("b (p j) t -> p b (j t)", j=PACK),
+                in_=result[:].rearrange("p b j t -> p b (j t)"),
             )
-            w_words = w_raw[:].bitcast(F32)
-            for first in range(0, CHUNK_PASSES, RUN_PASSES):
-                run = range(first, first + RUN_PASSES)
-                w_tiles = []
-                s_tiles = []
-                for c in run:
-                    w_grouped = grouped_pool.tile([P, CHANNELS * PACK], BF16, align_bytes=64, name="w_grouped")
-                    transpose_weights(nc, bank_pool, w_grouped, w_words, c * K_PASS // 2, ident)
-                    w_tiles.append(w_grouped)
-                for c in run:
-                    g = chunk * CHUNK_PASSES + c
-                    if g == FM_PASS:
-                        raw = fm_raw
-                    else:
-                        raw = raw_pool.tile([P, BATCH, PACK, TIMES], BF16, name="raw")
-                        source, first_channel = given_stream(g)
-                        load_stream_pass(nc, raw, source, first_channel)
-                    s_grouped = grouped_pool.tile([P, COLS * PACK], BF16, align_bytes=64, name="s_grouped")
-                    group_stream_words(nc, s_grouped, raw)
-                    s_tiles.append(s_grouped)
-                prepared = [
-                    (quantise(nc, operand_pool, w_tiles[n], "w"), quantise(nc, operand_pool, s_tiles[n], "s"))
-                    for n in range(RUN_PASSES)
-                ]
-                for weights, stream in waiting:
-                    multiply_pass(nc, z_sums, weights, stream, multiplied == 0, False)
-                    multiplied += 1
-                waiting = prepared
-        for weights, stream in waiting:
-            multiply_pass(nc, z_sums, weights, stream, False, multiplied == PASSES - 1)
-            multiplied += 1
-
-        result = work.tile([P, BATCH, PACK, TIMES], F32, name="result")
-        group_norm_relu(
-            nc, work, bank_pool, z_sums, group_mean,
-            vectors[:, 3, :], vectors[:, 4, :], vectors[:, 5, :], result[:],
-        )
-        nc.sync.dma_start(
-            out=out.rearrange("b (p j) t -> p b (j t)", j=PACK),
-            in_=result[:].rearrange("p b j t -> p b (j t)"),
-        )

@@ -22,7 +22,8 @@ CHANNELS = 512
 K_CAT = 16384
 PASSES = K_CAT // K_PASS
 FM_PASS = 3
-GROUP_VALUES = 16 * TIMES
+GROUP_ROWS = 16 * 2
+STATS = 6 * BATCH * PACK
 EPS = 1e-5
 
 CHUNK_PASSES = 4
@@ -97,18 +98,42 @@ def multiply_pass(nc, sums, weights, stream, start, stop):
         )
 
 
-def group_moments(nc, psum, work, row_sums, group_mean):
-    moments_psum = psum.tile([P, 2, BATCH], F32, tag="bank", name="moments_psum")
-    for j in range(PACK):
+def add_row_stats(nc, stats, y, j):
+    for b in range(BATCH):
+        first = (b * PACK + j) * 6
+        nc.vector.bn_stats(out=stats[:, first : first + 6], in_=y[:, j, b, :])
+
+
+def mean_squares(nc, work, stats):
+    means = stats[:, 1 : STATS : 3]
+    squares = work.tile([P, STATS // 3], F32, name="squares")
+    nc.vector.tensor_tensor(out=squares[:], in0=means, in1=means, op=ALU.mult)
+    nc.vector.scalar_tensor_tensor(
+        out=squares[:],
+        in0=stats[:, 2 : STATS : 3],
+        scalar=2.0 / TIMES,
+        in1=squares[:],
+        op0=ALU.mult,
+        op1=ALU.add,
+    )
+    return squares
+
+
+def group_variance(nc, psum, work, stats, squares, group_mean):
+    per_row = STATS // 3
+    sums = psum.tile([P, 2, per_row], F32, tag="bank", name="moment_sums")
+    for half, source in enumerate((stats[:, 1 : STATS : 3], squares[:])):
         nc.tensor.matmul(
-            out=moments_psum[:].rearrange("p s b -> p (s b)"),
+            out=sums[:, half, :],
             lhsT=group_mean[:].rearrange("p g r -> p (g r)"),
-            rhs=row_sums[:, j, :, :].rearrange("p s b -> p (s b)"),
-            start=(j == 0),
-            stop=(j == PACK - 1),
+            rhs=source,
+            start=True,
+            stop=True,
         )
     moments = work.tile([P, 2, BATCH], F32, name="moments")
-    nc.vector.tensor_copy(out=moments[:], in_=moments_psum[:])
+    nc.vector.tensor_reduce(
+        out=moments[:], in_=sums[:].rearrange("p s (b r) -> p s b r", b=BATCH), axis=AX.X, op=ALU.add
+    )
     var = work.tile([P, BATCH], F32, name="var")
     nc.vector.tensor_tensor(out=var[:], in0=moments[:, 0, :], in1=moments[:, 0, :], op=ALU.mult)
     nc.vector.tensor_tensor(out=var[:], in0=moments[:, 1, :], in1=var[:], op=ALU.subtract)
@@ -122,14 +147,18 @@ def square_root(nc, work, var):
     return std
 
 
-def normalise(nc, work, y, moments, std):
+def scale_and_shift(nc, work, moments, std):
     rstd = work.tile([P, BATCH], F32, name="rstd")
     shift = work.tile([P, BATCH], F32, name="shift")
     nc.vector.reciprocal(out=rstd[:], in_=std[:])
     nc.vector.scalar_tensor_tensor(
         out=shift[:], in0=moments[:, 0, :], scalar=-1.0, in1=rstd[:], op0=ALU.mult, op1=ALU.mult
     )
-    for b in range(BATCH):
+    return rstd, shift
+
+
+def normalise(nc, y, rstd, shift, batches):
+    for b in batches:
         nc.vector.tensor_scalar(
             out=y[:, :, b, :],
             in0=y[:, :, b, :],
@@ -140,15 +169,30 @@ def normalise(nc, work, y, moments, std):
         )
 
 
-def affine_relu(nc, y, gamma, beta, result):
-    for j in range(PACK):
+def affine_relu(nc, y, gamma, beta, result, tiles, batches):
+    for j in tiles:
         nc.scalar.activation(
-            out=result[:, :, j, :],
-            in_=y[:, j, :, :],
+            out=result[:, batches, j, :],
+            in_=y[:, j, batches, :],
             func=ACT.Relu,
             bias=beta[:, j : j + 1],
             scale=gamma[:, j : j + 1],
         )
+
+
+def affine_relu_on_vector(nc, y, gamma, beta, result, j, batches):
+    nc.vector.tensor_scalar(
+        out=y[:, j, batches, :],
+        in0=y[:, j, batches, :],
+        scalar1=gamma[:, j : j + 1],
+        scalar2=beta[:, j : j + 1],
+        op0=ALU.mult,
+        op1=ALU.add,
+    )
+    nc.vector.tensor_scalar(
+        out=result[:, batches, j, :], in0=y[:, j, batches, :], scalar1=0.0, scalar2=None, op0=ALU.max
+    )
+
 
 def tile_coarsepyramid_pc_k_kernel(
     tc,
@@ -178,7 +222,7 @@ def tile_coarsepyramid_pc_k_kernel(
     with ExitStack() as stack:
         const = stack.enter_context(tc.tile_pool(name="const", bufs=1))
         work = stack.enter_context(tc.tile_pool(name="work", bufs=1))
-        first_pool = stack.enter_context(tc.tile_pool(name="first_pool", bufs=2))
+        half_pool = stack.enter_context(tc.tile_pool(name="half_pool", bufs=2))
         w_pool = stack.enter_context(tc.tile_pool(name="w_pool", bufs=3))
         raw_pool = stack.enter_context(tc.tile_pool(name="raw_pool", bufs=10))
         grouped_pool = stack.enter_context(tc.tile_pool(name="grouped_pool", bufs=2 * RUN_PASSES))
@@ -199,7 +243,7 @@ def tile_coarsepyramid_pc_k_kernel(
         nc.vector.tensor_scalar(
             out=group_mean[:],
             in0=same_group[:].unsqueeze(2).to_broadcast([P, P // PACK, PACK]),
-            scalar1=1.0 / GROUP_VALUES,
+            scalar1=1.0 / GROUP_ROWS,
             scalar2=None,
             op0=ALU.mult,
         )
@@ -223,18 +267,7 @@ def tile_coarsepyramid_pc_k_kernel(
             for n, g in enumerate(passes):
                 w_words[g] = (words, n * K_PASS // 2)
 
-        def load_run(s):
-            if s >= len(runs):
-                return
-            if s == 0:
-                nc.sync.dma_start(out=w_cur_raw[:], in_=w_cur.rearrange("(p j) k -> p j k", j=PACK))
-                w_words[-1] = (w_cur_raw[:].bitcast(F32), 0)
-            elif s <= 2:
-                w_half = first_pool.tile([P, PACK, RUN_K], BF16, name="w_half")
-                load_weights(runs[s], w_half)
-            elif s % 2 == 1:
-                w_raw = w_pool.tile([P, PACK, CHUNK_K], BF16, name="w_raw")
-                load_weights(runs[s] + runs[s + 1], w_raw)
+        def load_streams(s):
             for g in runs[s]:
                 if g == FM_PASS:
                     raws[g] = fm_raw
@@ -246,6 +279,30 @@ def tile_coarsepyramid_pc_k_kernel(
                     source, first_channel = given_stream(g)
                     load_stream_pass(nc, raw, source, first_channel)
                 raws[g] = raw
+
+        last = len(runs) - 1
+        last_words = []
+
+        def load_run(s):
+            if s > last:
+                return
+            if s == 0:
+                nc.sync.dma_start(out=w_cur_raw[:], in_=w_cur.rearrange("(p j) k -> p j k", j=PACK))
+                w_words[-1] = (w_cur_raw[:].bitcast(F32), 0)
+            elif s in (1, 2, last - 1):
+                w_half = half_pool.tile([P, PACK, RUN_K], BF16, name="w_half")
+                load_weights(runs[s], w_half)
+            elif s % 2 == 1:
+                w_raw = w_pool.tile([P, PACK, CHUNK_K], BF16, name="w_raw")
+                load_weights(runs[s] + runs[s + 1], w_raw)
+            load_streams(s)
+            if s == last:
+                k0 = runs[s][0] * K_PASS
+                rows = w_prop.rearrange("(p j) k -> p j k", j=PACK)
+                for j in range(PACK):
+                    w_tile = half_pool.tile([P, RUN_K], BF16, name="w_tile%d" % j)
+                    nc.sync.dma_start(out=w_tile[:], in_=rows[:, j, k0 : k0 + RUN_K])
+                    last_words.append(w_tile[:].bitcast(F32))
 
         PREFETCH = 4
         for s in range(PREFETCH):
@@ -279,46 +336,91 @@ def tile_coarsepyramid_pc_k_kernel(
                 transpose_weights(nc, bank_pool, grouped, words, first_word, ident)
                 w_grouped[g] = grouped
 
-        def quantise_run(s):
+        def quantise_streams(s):
             for g in runs[s]:
                 operands[g] = [None, quantise(nc, operand_pool, s_grouped[g], "s")]
+
+        def quantise_weights(s):
             for g in runs[s]:
                 operands[g][0] = quantise(nc, operand_pool, w_grouped[g], "w")
+
+        tile_grouped = []
+        tile_operands = []
+
+        def transpose_last(j):
+            grouped = grouped_pool.tile([P, RUN_PASSES * P * PACK], BF16, align_bytes=64, name="tile_grouped")
+            planes = bank_pool.tile([P, RUN_PASSES, 2, P], F32, tag="bank", name="tile_planes")
+            for c in range(RUN_PASSES):
+                for u in range(2):
+                    first = c * K_PASS // 2 + u
+                    nc.tensor.transpose(
+                        planes[:, c, u, :], last_words[j][:, first : (c + 1) * K_PASS // 2 : 2], ident[:]
+                    )
+            nc.scalar.copy(
+                out=grouped[:].bitcast(F32).rearrange("q (c m u) -> q c m u", c=RUN_PASSES, u=2),
+                in_=planes[:].rearrange("q c u m -> q c m u"),
+            )
+            tile_grouped.append(grouped)
+
+        def quantise_last(j):
+            codes = operand_pool.tile([P, RUN_PASSES * P], U32, align_bytes=64, name="tile_codes")
+            scales = operand_pool.tile([P, RUN_PASSES * P], U8, align_bytes=64, name="tile_scales")
+            nc.vector.quantize_mx(out=codes[:].bitcast(FP8X4), scales=scales[:], in_=tile_grouped[j][:])
+            tile_operands.append((codes, scales))
+
+        def multiply_last(j):
+            codes, scales = tile_operands[j]
+            for c, g in enumerate(runs[last]):
+                s_codes, s_scales = operands[g][1]
+                rows = slice(c * P, (c + 1) * P)
+                nc.tensor.matmul_mx(
+                    out=sums[j][:],
+                    lhsT=codes[:, rows].bitcast(FP8X4),
+                    lhsT_scale=scales[:, rows],
+                    rhs=s_codes[:].bitcast(FP8X4),
+                    rhs_scale=s_scales[:],
+                    start=False,
+                    stop=(c == RUN_PASSES - 1),
+                )
 
         def new_sums():
             return [sums_pool.tile([P, COLS], F32, name="sums%d" % j) for j in range(PACK)]
 
         y = work.tile([P, PACK, BATCH, TIMES], F32, name="y")
-        squares = work.tile([P, PACK, BATCH, TIMES], F32, name="squares")
-        row_sums = work.tile([P, PACK, 2, BATCH], F32, name="row_sums")
+
+        def new_stats():
+            return work.tile([P, STATS], F32, name="stats")
 
         def flat(tile, j):
             return tile[:, j, :, :].rearrange("p b t -> p (b t)")
 
-        def reduce_rows(source, j, s):
-            nc.vector.tensor_reduce(out=row_sums[:, j, s, :], in_=source[:, j, :, :], axis=AX.X, op=ALU.add)
+        def add_bias(j, vector):
+            nc.scalar.activation(
+                out=flat(y, j), in_=sums[j][:], func=ACT.Identity, bias=vectors[:, vector, j : j + 1]
+            )
 
+        every_b = slice(0, BATCH)
         with tc.manual_schedule():
             sums = new_sums()
+            stats = new_stats()
             multiplied = 0
             regroup(0)
-            for s in range(len(runs) + 1):
+            for s in range(last + 1):
                 load_run(s + PREFETCH)
                 if s == 2:
-                    for j in range(2):
-                        nc.scalar.activation(
-                            out=flat(y, j), in_=sums[j][:], func=ACT.Identity, bias=vectors[:, 0, j : j + 1]
-                        )
-                    for j in range(2, PACK):
-                        nc.vector.tensor_scalar(
-                            out=flat(y, j), in0=sums[j][:], scalar1=vectors[:, 0, j : j + 1], scalar2=None, op0=ALU.add
-                        )
+                    for j in range(PACK):
+                        if j < 2:
+                            add_bias(j, 0)
+                        else:
+                            nc.vector.tensor_scalar(
+                                out=flat(y, j), in0=sums[j][:], scalar1=vectors[:, 0, j : j + 1], scalar2=None, op0=ALU.add
+                            )
                     sums = new_sums()
-                if s == 7:
-                    moments, var = group_moments(nc, bank_pool, work, row_sums, group_mean)
-                if s < len(runs):
+                if s == 5:
+                    moments, var = group_variance(nc, bank_pool, work, stats, squares, group_mean)
+                if s < last:
                     transpose_run(s)
-                if s == 7:
+                if s == 5:
                     std = square_root(nc, work, var)
                 if s >= 1:
                     for g in runs[s - 1]:
@@ -326,38 +428,46 @@ def tile_coarsepyramid_pc_k_kernel(
                         if g < 0:
                             multiply_pass(nc, sums, weights, stream, True, True)
                         else:
-                            multiply_pass(nc, sums, weights, stream, multiplied == 0, multiplied == PASSES - 1)
+                            multiply_pass(nc, sums, weights, stream, multiplied == 0, False)
                             multiplied += 1
                 if s in (3, 4):
                     for j in (2 * s - 6, 2 * s - 5):
-                        reduce_rows(y, j, 0)
-                        nc.scalar.activation(out=flat(squares, j), in_=flat(y, j), func=ACT.Square)
-                if s in (5, 6):
-                    for j in (2 * s - 10, 2 * s - 9):
-                        reduce_rows(squares, j, 1)
-                if s == 8:
-                    normalise(nc, work, y, moments, std)
+                        add_row_stats(nc, stats, y, j)
+                if s == 4:
+                    squares = mean_squares(nc, work, stats)
+                if s == 6:
+                    rstd, shift = scale_and_shift(nc, work, moments, std)
+                    normalise(nc, y, rstd, shift, range(BATCH))
                 regroup(s + 1)
-                if s == 8:
-                    affine_relu(nc, y, vectors[:, 1, :], vectors[:, 2, :], fm_raw)
-                if s < len(runs):
-                    quantise_run(s)
+                if s in (6, 7):
+                    affine_relu(
+                        nc, y, vectors[:, 1, :], vectors[:, 2, :], fm_raw, (2 * s - 12, 2 * s - 11), every_b
+                    )
+                quantise_streams(s)
+                if s < last:
+                    quantise_weights(s)
 
+            stats = new_stats()
             for j in range(PACK):
-                nc.scalar.activation(
-                    out=flat(y, j), in_=sums[j][:], func=ACT.Identity, bias=vectors[:, 3, j : j + 1]
-                )
-                nc.scalar.activation(
-                    out=flat(squares, j), in_=sums[j][:], func=ACT.Square, bias=vectors[:, 3, j : j + 1]
-                )
-                reduce_rows(y, j, 0)
-                reduce_rows(squares, j, 1)
-            moments, var = group_moments(nc, bank_pool, work, row_sums, group_mean)
+                transpose_last(j)
+                quantise_last(j)
+                if j > 0:
+                    multiply_last(j - 1)
+                    add_bias(j - 1, 3)
+            multiply_last(PACK - 1)
+            add_bias(PACK - 1, 3)
+            for j in range(PACK):
+                add_row_stats(nc, stats, y, j)
+            squares = mean_squares(nc, work, stats)
+            moments, var = group_variance(nc, bank_pool, work, stats, squares, group_mean)
             std = square_root(nc, work, var)
-            normalise(nc, work, y, moments, std)
+            rstd, shift = scale_and_shift(nc, work, moments, std)
             result = work.tile([P, BATCH, PACK, TIMES], F32, name="result")
-            affine_relu(nc, y, vectors[:, 4, :], vectors[:, 5, :], result)
-            nc.sync.dma_start(
-                out=out.rearrange("b (p j) t -> p b (j t)", j=PACK),
-                in_=result[:].rearrange("p b j t -> p b (j t)"),
-            )
+            for batches in (slice(0, BATCH // 2), slice(BATCH // 2, BATCH)):
+                normalise(nc, y, rstd, shift, range(batches.start, batches.stop))
+                affine_relu(nc, y, vectors[:, 4, :], vectors[:, 5, :], result, range(PACK - 1), batches)
+                affine_relu_on_vector(nc, y, vectors[:, 4, :], vectors[:, 5, :], result, PACK - 1, batches)
+                nc.sync.dma_start(
+                    out=out[batches, :, :].rearrange("b (p j) t -> p b (j t)", j=PACK),
+                    in_=result[:, batches, :, :].rearrange("p b j t -> p b (j t)"),
+                )

@@ -329,12 +329,11 @@ def tile_coarsepyramid_pc_k_kernel(
                 group_on_scalar(nc, grouped, raws[g])
                 s_grouped[g] = grouped
 
-        def transpose_run(s):
-            for g in runs[s]:
-                grouped = grouped_pool.tile([P, CHANNELS * PACK], BF16, align_bytes=64, name="w_grouped")
-                words, first_word = w_words[g]
-                transpose_weights(nc, bank_pool, grouped, words, first_word, ident)
-                w_grouped[g] = grouped
+        def transpose_pass(g):
+            grouped = grouped_pool.tile([P, CHANNELS * PACK], BF16, align_bytes=64, name="w_grouped")
+            words, first_word = w_words[g]
+            transpose_weights(nc, bank_pool, grouped, words, first_word, ident)
+            w_grouped[g] = grouped
 
         def quantise_streams(s):
             for g in runs[s]:
@@ -418,18 +417,19 @@ def tile_coarsepyramid_pc_k_kernel(
                     sums = new_sums()
                 if s == 5:
                     moments, var = group_variance(nc, bank_pool, work, stats, squares, group_mean)
-                if s < last:
-                    transpose_run(s)
-                if s == 5:
-                    std = square_root(nc, work, var)
-                if s >= 1:
-                    for g in runs[s - 1]:
+                for n in range(RUN_PASSES):
+                    if s < last and n < len(runs[s]):
+                        transpose_pass(runs[s][n])
+                    if s >= 1 and n < len(runs[s - 1]):
+                        g = runs[s - 1][n]
                         weights, stream = operands[g][0], operands[g][1]
                         if g < 0:
                             multiply_pass(nc, sums, weights, stream, True, True)
                         else:
                             multiply_pass(nc, sums, weights, stream, multiplied == 0, False)
                             multiplied += 1
+                if s == 5:
+                    std = square_root(nc, work, var)
                 if s in (3, 4):
                     for j in (2 * s - 6, 2 * s - 5):
                         add_row_stats(nc, stats, y, j)

@@ -30,8 +30,9 @@ CHUNK_PASSES = 4
 CHUNK_K = CHUNK_PASSES * K_PASS
 RUN_PASSES = 2
 RUN_K = RUN_PASSES * K_PASS
+HEAD = 4
 VECTOR_TIMES = 40
-CHUNK_ORDER = (1, 2, 3, 4, 0, 5, 6, 7)
+CHUNK_ORDER = (1, 2, 3, 4, 5, 0, 6, 7)
 
 FLOPS = 2 * COLS * CHANNELS * (CHANNELS + K_CAT)
 
@@ -65,10 +66,9 @@ def transpose_weights(nc, psum, grouped, words, first_word, ident):
         planes = psum.tile([P, 2, 2 * P], F32, tag="bank", name="planes")
         for u in range(2):
             for i in range(2):
+                columns = slice(first_word + u, first_word + 2 * P, 2)
                 nc.tensor.transpose(
-                    planes[:, u, i * P : (i + 1) * P],
-                    words[:, 2 * half + i, first_word + u : first_word + 2 * P : 2],
-                    ident[:],
+                    planes[:, u, i * P : (i + 1) * P], words[:, 2 * half + i, columns], ident[:]
                 )
         nc.scalar.copy(
             out=grouped_words[:, half * 2 * P : (half + 1) * 2 * P, :],
@@ -119,9 +119,8 @@ def mean_squares(nc, work, stats):
     return squares
 
 
-def group_variance(nc, psum, work, stats, squares, group_mean):
-    per_row = STATS // 3
-    sums = psum.tile([P, 2, per_row], F32, tag="bank", name="moment_sums")
+def group_sums(nc, psum, stats, squares, group_mean):
+    sums = psum.tile([P, 2, STATS // 3], F32, tag="bank", name="moment_sums")
     for half, source in enumerate((stats[:, 1 : STATS : 3], squares[:])):
         nc.tensor.matmul(
             out=sums[:, half, :],
@@ -130,6 +129,10 @@ def group_variance(nc, psum, work, stats, squares, group_mean):
             start=True,
             stop=True,
         )
+    return sums
+
+
+def group_moments(nc, work, sums):
     moments = work.tile([P, 2, BATCH], F32, name="moments")
     nc.vector.tensor_reduce(
         out=moments[:], in_=sums[:].rearrange("p s (b r) -> p s b r", b=BATCH), axis=AX.X, op=ALU.add
@@ -180,7 +183,7 @@ def affine_relu(nc, y, gamma, beta, result, tiles, batches):
         )
 
 
-def affine_relu_on_vector(nc, y, gamma, beta, result, j, batches):
+def affine_on_vector(nc, y, gamma, beta, j, batches):
     nc.vector.tensor_scalar(
         out=y[:, j, batches, :],
         in0=y[:, j, batches, :],
@@ -189,6 +192,9 @@ def affine_relu_on_vector(nc, y, gamma, beta, result, j, batches):
         op0=ALU.mult,
         op1=ALU.add,
     )
+
+
+def relu_on_vector(nc, y, result, j, batches):
     nc.vector.tensor_scalar(
         out=result[:, batches, j, :], in0=y[:, j, batches, :], scalar1=0.0, scalar2=None, op0=ALU.max
     )
@@ -222,13 +228,21 @@ def tile_coarsepyramid_pc_k_kernel(
     with ExitStack() as stack:
         const = stack.enter_context(tc.tile_pool(name="const", bufs=1))
         work = stack.enter_context(tc.tile_pool(name="work", bufs=1))
-        half_pool = stack.enter_context(tc.tile_pool(name="half_pool", bufs=2))
-        w_pool = stack.enter_context(tc.tile_pool(name="w_pool", bufs=3))
-        raw_pool = stack.enter_context(tc.tile_pool(name="raw_pool", bufs=10))
-        grouped_pool = stack.enter_context(tc.tile_pool(name="grouped_pool", bufs=2 * RUN_PASSES))
-        operand_pool = stack.enter_context(tc.tile_pool(name="operand_pool", bufs=3 * RUN_PASSES))
+        single_pool = stack.enter_context(tc.tile_pool(name="single_pool", bufs=2))
+        half_pool = stack.enter_context(tc.tile_pool(name="half_pool", bufs=4))
+        tile_pool = stack.enter_context(tc.tile_pool(name="tile_pool", bufs=PACK))
+        raw_pool = stack.enter_context(tc.tile_pool(name="raw_pool", bufs=12))
+        grouped_pool = stack.enter_context(tc.tile_pool(name="grouped_pool", bufs=3))
+        operand_pool = stack.enter_context(tc.tile_pool(name="operand_pool", bufs=5))
         sums_pool = stack.enter_context(tc.psum_pool(name="sums_pool", bufs=1))
         bank_pool = stack.enter_context(tc.psum_pool(name="bank_pool", bufs=4))
+
+        vectors_bf16 = const.tile([P, 6, 16], BF16)
+        for v, vector in enumerate((b_cur, g_cur, be_cur, b_prop, g_prop, be_prop)):
+            nc.scalar.dma_start(
+                out=vectors_bf16[:, v, 0:PACK], in_=vector.rearrange("(p j) -> p j", j=PACK)
+            )
+        vectors = const.tile([P, 6, PACK], F32)
 
         one = const.tile([P, 1], F32)
         nc.vector.memset(one[:], 1.0)
@@ -248,106 +262,110 @@ def tile_coarsepyramid_pc_k_kernel(
             op0=ALU.mult,
         )
 
-        runs = [[-1]]
-        for chunk in CHUNK_ORDER:
-            for first in range(0, CHUNK_PASSES, RUN_PASSES):
-                runs.append([chunk * CHUNK_PASSES + first + n for n in range(RUN_PASSES)])
+        Y_PASS = -1
+        order = [Y_PASS] + [
+            chunk * CHUNK_PASSES + c for chunk in CHUNK_ORDER for c in range(CHUNK_PASSES)
+        ]
+        steps = len(order) - RUN_PASSES
+        last_pair = order[steps:]
         w_words = {}
         raws = {}
         w_cur_raw = const.tile([P, PACK, K_PASS], BF16)
         fm_raw = const.tile([P, BATCH, PACK, TIMES], BF16)
+        last_words = []
 
-        def load_weights(passes, tile):
+        def load_weights(first, count):
+            passes = order[first : first + count]
             k0 = passes[0] * K_PASS
+            pool = {1: single_pool, 2: half_pool}[count]
+            w_raw = pool.tile([P, PACK, count * K_PASS], BF16, name="w_raw%d" % count)
             nc.sync.dma_start(
-                out=tile[:],
-                in_=w_prop[:, k0 : k0 + len(passes) * K_PASS].rearrange("(p j) k -> p j k", j=PACK),
+                out=w_raw[:],
+                in_=w_prop[:, k0 : k0 + count * K_PASS].rearrange("(p j) k -> p j k", j=PACK),
             )
-            words = tile[:].bitcast(F32)
+            words = w_raw[:].bitcast(F32)
             for n, g in enumerate(passes):
                 w_words[g] = (words, n * K_PASS // 2)
 
-        def load_streams(s):
-            for g in runs[s]:
-                if g == FM_PASS:
-                    raws[g] = fm_raw
-                    continue
-                raw = raw_pool.tile([P, BATCH, PACK, TIMES], BF16, name="raw")
-                if g < 0:
-                    load_stream_pass(nc, raw, feature, 0)
-                else:
-                    source, first_channel = given_stream(g)
-                    load_stream_pass(nc, raw, source, first_channel)
-                raws[g] = raw
 
-        last = len(runs) - 1
-        last_words = []
-
-        def load_run(s):
-            if s > last:
+        def load(n):
+            if n >= len(order):
                 return
-            if s == 0:
+            g = order[n]
+            if n == 0:
                 nc.sync.dma_start(out=w_cur_raw[:], in_=w_cur.rearrange("(p j) k -> p j k", j=PACK))
-                w_words[-1] = (w_cur_raw[:].bitcast(F32), 0)
-            elif s in (1, 2, last - 1):
-                w_half = half_pool.tile([P, PACK, RUN_K], BF16, name="w_half")
-                load_weights(runs[s], w_half)
-            elif s % 2 == 1:
-                w_raw = w_pool.tile([P, PACK, CHUNK_K], BF16, name="w_raw")
-                load_weights(runs[s] + runs[s + 1], w_raw)
-            load_streams(s)
-            if s == last:
-                k0 = runs[s][0] * K_PASS
+                w_words[g] = (w_cur_raw[:].bitcast(F32), 0)
+            if n in (1, 2):
+                load_weights(n, 1)
+            elif n % 2 == 1 and n < steps:
+                load_weights(n, 2)
+            if g == FM_PASS:
+                raws[g] = fm_raw
+            else:
+                raw = raw_pool.tile([P, BATCH, PACK, TIMES], BF16, name="raw")
+                source, first_channel = (feature, 0) if n == 0 else given_stream(g)
+                load_stream_pass(nc, raw, source, first_channel)
+                raws[g] = raw
+            if n == len(order) - 1:
+                k0 = last_pair[0] * K_PASS
                 rows = w_prop.rearrange("(p j) k -> p j k", j=PACK)
                 for j in range(PACK):
-                    w_tile = half_pool.tile([P, RUN_K], BF16, name="w_tile%d" % j)
+                    w_tile = work.tile([P, RUN_K], BF16, name="w_tile%d" % j)
                     nc.sync.dma_start(out=w_tile[:], in_=rows[:, j, k0 : k0 + RUN_K])
                     last_words.append(w_tile[:].bitcast(F32))
 
-        PREFETCH = 4
-        for s in range(PREFETCH):
-            load_run(s)
-
-        vectors_bf16 = const.tile([P, 6, 16], BF16)
-        for v, vector in enumerate((b_cur, g_cur, be_cur, b_prop, g_prop, be_prop)):
-            nc.scalar.dma_start(
-                out=vectors_bf16[:, v, 0:PACK], in_=vector.rearrange("(p j) -> p j", j=PACK)
-            )
-        vectors = const.tile([P, 6, PACK], F32)
-        nc.vector.tensor_copy(out=vectors[:], in_=vectors_bf16[:, :, 0:PACK])
-
         s_grouped = {}
         w_grouped = {}
-        operands = {}
+        stream_operands = {}
+        weight_operands = {}
 
-        def regroup(s):
-            if s >= len(runs):
-                return
-            for g in runs[s]:
+        def regroup(n):
+            if n < len(order):
+                g = order[n]
                 grouped = grouped_pool.tile([P, COLS * PACK], BF16, align_bytes=64, name="s_grouped")
                 group_on_vector(nc, grouped, raws[g])
                 group_on_scalar(nc, grouped, raws[g])
                 s_grouped[g] = grouped
 
-        def transpose_pass(g):
+        def quantise_stream(n):
+            if n < len(order):
+                g = order[n]
+                stream_operands[g] = quantise(nc, operand_pool, s_grouped[g], "s")
+
+        def transpose_pass(n):
+            g = order[n]
             grouped = grouped_pool.tile([P, CHANNELS * PACK], BF16, align_bytes=64, name="w_grouped")
             words, first_word = w_words[g]
             transpose_weights(nc, bank_pool, grouped, words, first_word, ident)
             w_grouped[g] = grouped
 
-        def quantise_streams(s):
-            for g in runs[s]:
-                operands[g] = [None, quantise(nc, operand_pool, s_grouped[g], "s")]
+        def quantise_weights(n):
+            g = order[n]
+            weight_operands[g] = quantise(nc, operand_pool, w_grouped[g], "w")
 
-        def quantise_weights(s):
-            for g in runs[s]:
-                operands[g][0] = quantise(nc, operand_pool, w_grouped[g], "w")
+        def multiply(n):
+            g = order[n]
+            multiply_pass(nc, sums, weight_operands[g], stream_operands[g], n <= 1, n == 0)
+
+        def multiply_tile(n, j):
+            w_codes, w_scales = weight_operands[order[n]]
+            s_codes, s_scales = stream_operands[order[n]]
+            rows = slice(j * P, (j + 1) * P)
+            nc.tensor.matmul_mx(
+                out=sums[j][:],
+                lhsT=w_codes[:, rows].bitcast(FP8X4),
+                lhsT_scale=w_scales[:, rows],
+                rhs=s_codes[:].bitcast(FP8X4),
+                rhs_scale=s_scales[:],
+                start=False,
+                stop=False,
+            )
 
         tile_grouped = []
         tile_operands = []
 
         def transpose_last(j):
-            grouped = grouped_pool.tile([P, RUN_PASSES * P * PACK], BF16, align_bytes=64, name="tile_grouped")
+            grouped = tile_pool.tile([P, RUN_PASSES * P * PACK], BF16, align_bytes=64, name="tile_grouped")
             planes = bank_pool.tile([P, RUN_PASSES, 2, P], F32, tag="bank", name="tile_planes")
             for c in range(RUN_PASSES):
                 for u in range(2):
@@ -362,15 +380,15 @@ def tile_coarsepyramid_pc_k_kernel(
             tile_grouped.append(grouped)
 
         def quantise_last(j):
-            codes = operand_pool.tile([P, RUN_PASSES * P], U32, align_bytes=64, name="tile_codes")
-            scales = operand_pool.tile([P, RUN_PASSES * P], U8, align_bytes=64, name="tile_scales")
+            codes = tile_pool.tile([P, RUN_PASSES * P], U32, align_bytes=64, name="tile_codes")
+            scales = tile_pool.tile([P, RUN_PASSES * P], U8, align_bytes=64, name="tile_scales")
             nc.vector.quantize_mx(out=codes[:].bitcast(FP8X4), scales=scales[:], in_=tile_grouped[j][:])
             tile_operands.append((codes, scales))
 
         def multiply_last(j):
             codes, scales = tile_operands[j]
-            for c, g in enumerate(runs[last]):
-                s_codes, s_scales = operands[g][1]
+            for c, g in enumerate(last_pair):
+                s_codes, s_scales = stream_operands[g]
                 rows = slice(c * P, (c + 1) * P)
                 nc.tensor.matmul_mx(
                     out=sums[j][:],
@@ -398,76 +416,84 @@ def tile_coarsepyramid_pc_k_kernel(
                 out=flat(y, j), in_=sums[j][:], func=ACT.Identity, bias=vectors[:, vector, j : j + 1]
             )
 
+        def evacuate():
+            nc.vector.tensor_copy(out=vectors[:], in_=vectors_bf16[:, :, 0:PACK])
+            for j in range(PACK):
+                if j < 2:
+                    add_bias(j, 0)
+                else:
+                    nc.vector.tensor_scalar(
+                        out=flat(y, j), in0=sums[j][:], scalar1=vectors[:, 0, j : j + 1], scalar2=None, op0=ALU.add
+                    )
+
         every_b = slice(0, BATCH)
+        PREFETCH = 9
+        for n in range(PREFETCH):
+            load(n)
+        G0 = 5
         with tc.manual_schedule():
             sums = new_sums()
             stats = new_stats()
-            multiplied = 0
             regroup(0)
-            for s in range(last + 1):
-                load_run(s + PREFETCH)
-                if s == 2:
-                    for j in range(PACK):
-                        if j < 2:
-                            add_bias(j, 0)
-                        else:
-                            nc.vector.tensor_scalar(
-                                out=flat(y, j), in0=sums[j][:], scalar1=vectors[:, 0, j : j + 1], scalar2=None, op0=ALU.add
-                            )
+            for n in range(steps):
+                load(n + PREFETCH)
+                transpose_pass(n)
+                if n >= 2:
+                    multiply(n - 2)
+                if n == 2:
+                    evacuate()
                     sums = new_sums()
-                if s == 5:
-                    moments, var = group_variance(nc, bank_pool, work, stats, squares, group_mean)
-                for n in range(RUN_PASSES):
-                    if s < last and n < len(runs[s]):
-                        transpose_pass(runs[s][n])
-                    if s >= 1 and n < len(runs[s - 1]):
-                        g = runs[s - 1][n]
-                        weights, stream = operands[g][0], operands[g][1]
-                        if g < 0:
-                            multiply_pass(nc, sums, weights, stream, True, True)
-                        else:
-                            multiply_pass(nc, sums, weights, stream, multiplied == 0, False)
-                            multiplied += 1
-                if s == 5:
-                    std = square_root(nc, work, var)
-                if s in (3, 4):
-                    for j in (2 * s - 6, 2 * s - 5):
-                        add_row_stats(nc, stats, y, j)
-                if s == 4:
+                quantise_stream(n)
+                if G0 <= n < G0 + PACK:
+                    add_row_stats(nc, stats, y, n - G0)
+                if n == G0 + 4:
                     squares = mean_squares(nc, work, stats)
-                if s == 6:
+                    moment_sums = group_sums(nc, bank_pool, stats, squares, group_mean)
+                if n == G0 + 6:
+                    std = square_root(nc, work, var)
+                if n == G0 + 7:
                     rstd, shift = scale_and_shift(nc, work, moments, std)
-                    normalise(nc, y, rstd, shift, range(BATCH))
-                regroup(s + 1)
-                if s in (6, 7):
-                    affine_relu(
-                        nc, y, vectors[:, 1, :], vectors[:, 2, :], fm_raw, (2 * s - 12, 2 * s - 11), every_b
-                    )
-                quantise_streams(s)
-                if s < last:
-                    quantise_weights(s)
-
+                if n in (G0 + 7, G0 + 8):
+                    half = n - G0 - 7
+                    normalise(nc, y, rstd, shift, range(half * 4, half * 4 + 4))
+                regroup(n + 1)
+                if G0 + 9 <= n < G0 + 9 + PACK:
+                    affine_relu(nc, y, vectors[:, 1, :], vectors[:, 2, :], fm_raw, (n - G0 - 9,), every_b)
+                if n >= 1:
+                    quantise_weights(n - 1)
+                if n == G0 + 5:
+                    moments, var = group_moments(nc, work, moment_sums)
             stats = new_stats()
+            multiply(steps - 2)
+            regroup(steps + 1)
+            quantise_stream(steps)
+            quantise_weights(steps - 1)
+            quantise_stream(steps + 1)
             for j in range(PACK):
                 transpose_last(j)
                 quantise_last(j)
-                if j > 0:
-                    multiply_last(j - 1)
-                    add_bias(j - 1, 3)
-            multiply_last(PACK - 1)
-            add_bias(PACK - 1, 3)
             for j in range(PACK):
+                multiply_tile(steps - 1, j)
+                multiply_last(j)
+                add_bias(j, 3)
                 add_row_stats(nc, stats, y, j)
             squares = mean_squares(nc, work, stats)
-            moments, var = group_variance(nc, bank_pool, work, stats, squares, group_mean)
+            moment_sums = group_sums(nc, bank_pool, stats, squares, group_mean)
+            moments, var = group_moments(nc, work, moment_sums)
             std = square_root(nc, work, var)
             rstd, shift = scale_and_shift(nc, work, moments, std)
             result = work.tile([P, BATCH, PACK, TIMES], F32, name="result")
-            for batches in (slice(0, BATCH // 2), slice(BATCH // 2, BATCH)):
-                normalise(nc, y, rstd, shift, range(batches.start, batches.stop))
-                affine_relu(nc, y, vectors[:, 4, :], vectors[:, 5, :], result, range(PACK - 1), batches)
-                affine_relu_on_vector(nc, y, vectors[:, 4, :], vectors[:, 5, :], result, PACK - 1, batches)
-                nc.sync.dma_start(
-                    out=out[batches, :, :].rearrange("b (p j) t -> p b (j t)", j=PACK),
-                    in_=result[:, batches, :, :].rearrange("p b j t -> p b (j t)"),
-                )
+            quarters = [slice(first, first + 2) for first in range(0, BATCH, 2)]
+            for q in range(len(quarters) + 2):
+                if q < len(quarters):
+                    normalise(nc, y, rstd, shift, range(2 * q, 2 * q + 2))
+                    affine_relu(nc, y, vectors[:, 4, :], vectors[:, 5, :], result, range(PACK - 1), quarters[q])
+                if 1 <= q <= len(quarters):
+                    affine_on_vector(nc, y, vectors[:, 4, :], vectors[:, 5, :], PACK - 1, quarters[q - 1])
+                if q >= 2:
+                    batches = quarters[q - 2]
+                    relu_on_vector(nc, y, result, PACK - 1, batches)
+                    nc.sync.dma_start(
+                        out=out[batches, :, :].rearrange("b (p j) t -> p b (j t)", j=PACK),
+                        in_=result[:, batches, :, :].rearrange("p b j t -> p b (j t)"),
+                    )

@@ -23,15 +23,14 @@ K_CAT = 16384
 PASSES = K_CAT // K_PASS
 FM_PASS = 3
 GROUP_ROWS = 16 * 2
-STATS = 6 * BATCH * PACK
 EPS = 1e-5
 
 CHUNK_PASSES = 4
-CHUNK_K = CHUNK_PASSES * K_PASS
 RUN_PASSES = 2
 RUN_K = RUN_PASSES * K_PASS
-HEAD = 4
-VECTOR_TIMES = 40
+VECTOR_TIMES = 48
+LAG = 2
+GROUP_NORM_STEP = 5
 CHUNK_ORDER = (1, 2, 3, 4, 5, 0, 6, 7)
 
 FLOPS = 2 * COLS * CHANNELS * (CHANNELS + K_CAT)
@@ -98,44 +97,49 @@ def multiply_pass(nc, sums, weights, stream, start, stop):
         )
 
 
-def add_row_stats(nc, stats, y, j):
+def add_row_stats(nc, stats, source, j):
     for b in range(BATCH):
-        first = (b * PACK + j) * 6
-        nc.vector.bn_stats(out=stats[:, first : first + 6], in_=y[:, j, b, :])
+        nc.vector.bn_stats(
+            out=stats[:, j, b, :, :].rearrange("p e s -> p (e s)"), in_=source[:, b * TIMES : (b + 1) * TIMES]
+        )
 
 
-def mean_squares(nc, work, stats):
-    means = stats[:, 1 : STATS : 3]
-    squares = work.tile([P, STATS // 3], F32, name="squares")
-    nc.vector.tensor_tensor(out=squares[:], in0=means, in1=means, op=ALU.mult)
+def half_row_moments(nc, row_moments, stats, bias):
+    mean = row_moments[:, 0, :, :, :].rearrange("p j b e -> p j (b e)")
+    mean_of_squares = row_moments[:, 1, :, :, :].rearrange("p j b e -> p j (b e)")
+    nc.vector.tensor_tensor(
+        out=mean,
+        in0=stats[:, :, :, :, 1].rearrange("p j b e -> p j (b e)"),
+        in1=bias.unsqueeze(2).to_broadcast([P, PACK, 2 * BATCH]),
+        op=ALU.add,
+    )
+    nc.vector.tensor_tensor(out=mean_of_squares, in0=mean, in1=mean, op=ALU.mult)
     nc.vector.scalar_tensor_tensor(
-        out=squares[:],
-        in0=stats[:, 2 : STATS : 3],
+        out=mean_of_squares,
+        in0=stats[:, :, :, :, 2].rearrange("p j b e -> p j (b e)"),
         scalar=2.0 / TIMES,
-        in1=squares[:],
+        in1=mean_of_squares,
         op0=ALU.mult,
         op1=ALU.add,
     )
-    return squares
 
 
-def group_sums(nc, psum, stats, squares, group_mean):
-    sums = psum.tile([P, 2, STATS // 3], F32, tag="bank", name="moment_sums")
-    for half, source in enumerate((stats[:, 1 : STATS : 3], squares[:])):
-        nc.tensor.matmul(
-            out=sums[:, half, :],
-            lhsT=group_mean[:].rearrange("p g r -> p (g r)"),
-            rhs=source,
-            start=True,
-            stop=True,
-        )
+def add_groups(nc, psum, row_moments, group_mean):
+    sums = psum.tile([P, 2, PACK, BATCH, 2], F32, tag="bank", name="moment_sums")
+    nc.tensor.matmul(
+        out=sums[:].rearrange("p s j b e -> p (s j b e)"),
+        lhsT=group_mean[:].rearrange("p g r -> p (g r)"),
+        rhs=row_moments[:].rearrange("p s j b e -> p (s j b e)"),
+        start=True,
+        stop=True,
+    )
     return sums
 
 
 def group_moments(nc, work, sums):
     moments = work.tile([P, 2, BATCH], F32, name="moments")
     nc.vector.tensor_reduce(
-        out=moments[:], in_=sums[:].rearrange("p s (b r) -> p s b r", b=BATCH), axis=AX.X, op=ALU.add
+        out=moments[:], in_=sums[:].rearrange("p s j b e -> p s b j e"), axis=AX.XY, op=ALU.add
     )
     var = work.tile([P, BATCH], F32, name="var")
     nc.vector.tensor_tensor(out=var[:], in0=moments[:, 0, :], in1=moments[:, 0, :], op=ALU.mult)
@@ -150,25 +154,21 @@ def square_root(nc, work, var):
     return std
 
 
-def scale_and_shift(nc, work, moments, std):
+def reciprocal(nc, work, std):
     rstd = work.tile([P, BATCH], F32, name="rstd")
-    shift = work.tile([P, BATCH], F32, name="shift")
     nc.vector.reciprocal(out=rstd[:], in_=std[:])
-    nc.vector.scalar_tensor_tensor(
-        out=shift[:], in0=moments[:, 0, :], scalar=-1.0, in1=rstd[:], op0=ALU.mult, op1=ALU.mult
-    )
-    return rstd, shift
+    return rstd
 
 
-def normalise(nc, y, rstd, shift, batches):
+def normalise(nc, y, moments, rstd, batches):
     for b in batches:
         nc.vector.tensor_scalar(
             out=y[:, :, b, :],
             in0=y[:, :, b, :],
-            scalar1=rstd[:, b : b + 1],
-            scalar2=shift[:, b : b + 1],
-            op0=ALU.mult,
-            op1=ALU.add,
+            scalar1=moments[:, 0, b : b + 1],
+            scalar2=rstd[:, b : b + 1],
+            op0=ALU.subtract,
+            op1=ALU.mult,
         )
 
 
@@ -232,8 +232,8 @@ def tile_coarsepyramid_pc_k_kernel(
         half_pool = stack.enter_context(tc.tile_pool(name="half_pool", bufs=4))
         tile_pool = stack.enter_context(tc.tile_pool(name="tile_pool", bufs=PACK))
         raw_pool = stack.enter_context(tc.tile_pool(name="raw_pool", bufs=12))
-        grouped_pool = stack.enter_context(tc.tile_pool(name="grouped_pool", bufs=3))
-        operand_pool = stack.enter_context(tc.tile_pool(name="operand_pool", bufs=5))
+        grouped_pool = stack.enter_context(tc.tile_pool(name="grouped_pool", bufs=4))
+        operand_pool = stack.enter_context(tc.tile_pool(name="operand_pool", bufs=6))
         sums_pool = stack.enter_context(tc.psum_pool(name="sums_pool", bufs=1))
         bank_pool = stack.enter_context(tc.psum_pool(name="bank_pool", bufs=4))
 
@@ -247,6 +247,8 @@ def tile_coarsepyramid_pc_k_kernel(
         one = const.tile([P, 1], F32)
         nc.vector.memset(one[:], 1.0)
         nc.scalar.activation(out=one[:], in_=one[:], func=ACT.Sqrt)
+        no_bias = const.tile([P, PACK], F32)
+        nc.vector.memset(no_bias[:], 0.0)
         ident = const.tile([P, P], F32)
         make_identity(nc, ident[:])
         same_group = const.tile([P, P // PACK], F32)
@@ -405,8 +407,10 @@ def tile_coarsepyramid_pc_k_kernel(
 
         y = work.tile([P, PACK, BATCH, TIMES], F32, name="y")
 
-        def new_stats():
-            return work.tile([P, STATS], F32, name="stats")
+        def new_statistics():
+            stats = work.tile([P, PACK, BATCH, 2, 3], F32, name="stats")
+            row_moments = work.tile([P, 2, PACK, BATCH, 2], F32, name="row_moments")
+            return stats, row_moments
 
         def flat(tile, j):
             return tile[:, j, :, :].rearrange("p b t -> p (b t)")
@@ -416,58 +420,56 @@ def tile_coarsepyramid_pc_k_kernel(
                 out=flat(y, j), in_=sums[j][:], func=ACT.Identity, bias=vectors[:, vector, j : j + 1]
             )
 
-        def evacuate():
-            nc.vector.tensor_copy(out=vectors[:], in_=vectors_bf16[:, :, 0:PACK])
-            for j in range(PACK):
-                if j < 2:
-                    add_bias(j, 0)
-                else:
-                    nc.vector.tensor_scalar(
-                        out=flat(y, j), in0=sums[j][:], scalar1=vectors[:, 0, j : j + 1], scalar2=None, op0=ALU.add
-                    )
-
         every_b = slice(0, BATCH)
         PREFETCH = 9
         for n in range(PREFETCH):
             load(n)
-        G0 = 5
         with tc.manual_schedule():
             sums = new_sums()
-            stats = new_stats()
+            stats, row_moments = new_statistics()
             regroup(0)
             for n in range(steps):
                 load(n + PREFETCH)
                 transpose_pass(n)
-                if n >= 2:
-                    multiply(n - 2)
-                if n == 2:
-                    evacuate()
-                    sums = new_sums()
-                quantise_stream(n)
-                if G0 <= n < G0 + PACK:
-                    add_row_stats(nc, stats, y, n - G0)
-                if n == G0 + 4:
-                    squares = mean_squares(nc, work, stats)
-                    moment_sums = group_sums(nc, bank_pool, stats, squares, group_mean)
-                if n == G0 + 6:
-                    std = square_root(nc, work, var)
-                if n == G0 + 7:
-                    rstd, shift = scale_and_shift(nc, work, moments, std)
-                if n in (G0 + 7, G0 + 8):
-                    half = n - G0 - 7
-                    normalise(nc, y, rstd, shift, range(half * 4, half * 4 + 4))
-                regroup(n + 1)
-                if G0 + 9 <= n < G0 + 9 + PACK:
-                    affine_relu(nc, y, vectors[:, 1, :], vectors[:, 2, :], fm_raw, (n - G0 - 9,), every_b)
                 if n >= 1:
                     quantise_weights(n - 1)
-                if n == G0 + 5:
+                if n >= LAG:
+                    multiply(n - LAG)
+                if n == LAG:
+                    nc.vector.tensor_copy(out=vectors[:], in_=vectors_bf16[:, :, 0:PACK])
+                    for j in range(PACK):
+                        if j < 2:
+                            add_bias(j, 0)
+                        else:
+                            nc.vector.tensor_scalar(
+                                out=flat(y, j), in0=sums[j][:], scalar1=vectors[:, 0, j : j + 1], scalar2=None, op0=ALU.add
+                            )
+                    sums = new_sums()
+                quantise_stream(n)
+                regroup(n + 1)
+                g = n - GROUP_NORM_STEP
+                if 0 <= g < PACK:
+                    add_row_stats(nc, stats, flat(y, g), g)
+                if g == 4:
+                    half_row_moments(nc, row_moments, stats, no_bias[:])
+                if g == 5:
+                    moment_sums = add_groups(nc, bank_pool, row_moments, group_mean)
+                if g == 6:
                     moments, var = group_moments(nc, work, moment_sums)
-            stats = new_stats()
-            multiply(steps - 2)
-            regroup(steps + 1)
-            quantise_stream(steps)
+                if g == 7:
+                    std = square_root(nc, work, var)
+                if g == 8:
+                    rstd = reciprocal(nc, work, std)
+                if g in (8, 9):
+                    normalise(nc, y, moments, rstd, range(4 * g - 32, 4 * g - 28))
+                if 10 <= g < 10 + PACK:
+                    affine_relu(nc, y, vectors[:, 1, :], vectors[:, 2, :], fm_raw, (g - 10,), every_b)
             quantise_weights(steps - 1)
+            multiply(steps - 2)
+
+            stats, row_moments = new_statistics()
+            quantise_stream(steps)
+            regroup(steps + 1)
             quantise_stream(steps + 1)
             for j in range(PACK):
                 transpose_last(j)
@@ -475,23 +477,24 @@ def tile_coarsepyramid_pc_k_kernel(
             for j in range(PACK):
                 multiply_tile(steps - 1, j)
                 multiply_last(j)
+                add_row_stats(nc, stats, sums[j], j)
                 add_bias(j, 3)
-                add_row_stats(nc, stats, y, j)
-            squares = mean_squares(nc, work, stats)
-            moment_sums = group_sums(nc, bank_pool, stats, squares, group_mean)
+            half_row_moments(nc, row_moments, stats, vectors[:, 3, :])
+            moment_sums = add_groups(nc, bank_pool, row_moments, group_mean)
             moments, var = group_moments(nc, work, moment_sums)
             std = square_root(nc, work, var)
-            rstd, shift = scale_and_shift(nc, work, moments, std)
+            rstd = reciprocal(nc, work, std)
             result = work.tile([P, BATCH, PACK, TIMES], F32, name="result")
-            quarters = [slice(first, first + 2) for first in range(0, BATCH, 2)]
-            for q in range(len(quarters) + 2):
-                if q < len(quarters):
-                    normalise(nc, y, rstd, shift, range(2 * q, 2 * q + 2))
-                    affine_relu(nc, y, vectors[:, 4, :], vectors[:, 5, :], result, range(PACK - 1), quarters[q])
-                if 1 <= q <= len(quarters):
-                    affine_on_vector(nc, y, vectors[:, 4, :], vectors[:, 5, :], PACK - 1, quarters[q - 1])
+            gamma, beta = vectors[:, 4, :], vectors[:, 5, :]
+            pieces = [slice(0, 4), slice(4, 6), slice(6, 8)]
+            for q in range(len(pieces) + 2):
+                if q < len(pieces):
+                    normalise(nc, y, moments, rstd, range(pieces[q].start, pieces[q].stop))
+                    affine_relu(nc, y, gamma, beta, result, range(PACK - 1), pieces[q])
+                if 1 <= q <= len(pieces):
+                    affine_on_vector(nc, y, gamma, beta, PACK - 1, pieces[q - 1])
                 if q >= 2:
-                    batches = quarters[q - 2]
+                    batches = pieces[q - 2]
                     relu_on_vector(nc, y, result, PACK - 1, batches)
                     nc.sync.dma_start(
                         out=out[batches, :, :].rearrange("b (p j) t -> p b (j t)", j=PACK),

@@ -26,9 +26,7 @@ GROUP_ROWS = 16 * 2
 EPS = 1e-5
 
 CHUNK_PASSES = 4
-RUN_PASSES = 2
-RUN_K = RUN_PASSES * K_PASS
-VECTOR_TIMES = 48
+VECTOR_TIMES = 44
 LAG = 2
 GROUP_NORM_STEP = 5
 CHUNK_ORDER = (1, 2, 3, 4, 5, 0, 6, 7)
@@ -228,9 +226,7 @@ def tile_coarsepyramid_pc_k_kernel(
     with ExitStack() as stack:
         const = stack.enter_context(tc.tile_pool(name="const", bufs=1))
         work = stack.enter_context(tc.tile_pool(name="work", bufs=1))
-        single_pool = stack.enter_context(tc.tile_pool(name="single_pool", bufs=2))
-        half_pool = stack.enter_context(tc.tile_pool(name="half_pool", bufs=4))
-        tile_pool = stack.enter_context(tc.tile_pool(name="tile_pool", bufs=PACK))
+        w_pool = stack.enter_context(tc.tile_pool(name="w_pool", bufs=3))
         raw_pool = stack.enter_context(tc.tile_pool(name="raw_pool", bufs=12))
         grouped_pool = stack.enter_context(tc.tile_pool(name="grouped_pool", bufs=4))
         operand_pool = stack.enter_context(tc.tile_pool(name="operand_pool", bufs=6))
@@ -268,18 +264,16 @@ def tile_coarsepyramid_pc_k_kernel(
         order = [Y_PASS] + [
             chunk * CHUNK_PASSES + c for chunk in CHUNK_ORDER for c in range(CHUNK_PASSES)
         ]
-        steps = len(order) - RUN_PASSES
-        last_pair = order[steps:]
+        steps = len(order)
         w_words = {}
         raws = {}
         w_cur_raw = const.tile([P, PACK, K_PASS], BF16)
         fm_raw = const.tile([P, BATCH, PACK, TIMES], BF16)
-        last_words = []
 
         def load_weights(first, count):
             passes = order[first : first + count]
             k0 = passes[0] * K_PASS
-            pool = {1: single_pool, 2: half_pool}[count]
+            pool = w_pool
             w_raw = pool.tile([P, PACK, count * K_PASS], BF16, name="w_raw%d" % count)
             nc.sync.dma_start(
                 out=w_raw[:],
@@ -297,10 +291,8 @@ def tile_coarsepyramid_pc_k_kernel(
             if n == 0:
                 nc.sync.dma_start(out=w_cur_raw[:], in_=w_cur.rearrange("(p j) k -> p j k", j=PACK))
                 w_words[g] = (w_cur_raw[:].bitcast(F32), 0)
-            if n in (1, 2):
-                load_weights(n, 1)
-            elif n % 2 == 1 and n < steps:
-                load_weights(n, 2)
+            if n % 4 == 1:
+                load_weights(n, 4)
             if g == FM_PASS:
                 raws[g] = fm_raw
             else:
@@ -308,13 +300,6 @@ def tile_coarsepyramid_pc_k_kernel(
                 source, first_channel = (feature, 0) if n == 0 else given_stream(g)
                 load_stream_pass(nc, raw, source, first_channel)
                 raws[g] = raw
-            if n == len(order) - 1:
-                k0 = last_pair[0] * K_PASS
-                rows = w_prop.rearrange("(p j) k -> p j k", j=PACK)
-                for j in range(PACK):
-                    w_tile = work.tile([P, RUN_K], BF16, name="w_tile%d" % j)
-                    nc.sync.dma_start(out=w_tile[:], in_=rows[:, j, k0 : k0 + RUN_K])
-                    last_words.append(w_tile[:].bitcast(F32))
 
         s_grouped = {}
         w_grouped = {}
@@ -360,47 +345,8 @@ def tile_coarsepyramid_pc_k_kernel(
                 rhs=s_codes[:].bitcast(FP8X4),
                 rhs_scale=s_scales[:],
                 start=False,
-                stop=False,
+                stop=(n == steps - 1),
             )
-
-        tile_grouped = []
-        tile_operands = []
-
-        def transpose_last(j):
-            grouped = tile_pool.tile([P, RUN_PASSES * P * PACK], BF16, align_bytes=64, name="tile_grouped")
-            planes = bank_pool.tile([P, RUN_PASSES, 2, P], F32, tag="bank", name="tile_planes")
-            for c in range(RUN_PASSES):
-                for u in range(2):
-                    first = c * K_PASS // 2 + u
-                    nc.tensor.transpose(
-                        planes[:, c, u, :], last_words[j][:, first : (c + 1) * K_PASS // 2 : 2], ident[:]
-                    )
-            nc.scalar.copy(
-                out=grouped[:].bitcast(F32).rearrange("q (c m u) -> q c m u", c=RUN_PASSES, u=2),
-                in_=planes[:].rearrange("q c u m -> q c m u"),
-            )
-            tile_grouped.append(grouped)
-
-        def quantise_last(j):
-            codes = tile_pool.tile([P, RUN_PASSES * P], U32, align_bytes=64, name="tile_codes")
-            scales = tile_pool.tile([P, RUN_PASSES * P], U8, align_bytes=64, name="tile_scales")
-            nc.vector.quantize_mx(out=codes[:].bitcast(FP8X4), scales=scales[:], in_=tile_grouped[j][:])
-            tile_operands.append((codes, scales))
-
-        def multiply_last(j):
-            codes, scales = tile_operands[j]
-            for c, g in enumerate(last_pair):
-                s_codes, s_scales = stream_operands[g]
-                rows = slice(c * P, (c + 1) * P)
-                nc.tensor.matmul_mx(
-                    out=sums[j][:],
-                    lhsT=codes[:, rows].bitcast(FP8X4),
-                    lhsT_scale=scales[:, rows],
-                    rhs=s_codes[:].bitcast(FP8X4),
-                    rhs_scale=s_scales[:],
-                    start=False,
-                    stop=(c == RUN_PASSES - 1),
-                )
 
         def new_sums():
             return [sums_pool.tile([P, COLS], F32, name="sums%d" % j) for j in range(PACK)]
@@ -465,18 +411,11 @@ def tile_coarsepyramid_pc_k_kernel(
                 if 10 <= g < 10 + PACK:
                     affine_relu(nc, y, vectors[:, 1, :], vectors[:, 2, :], fm_raw, (g - 10,), every_b)
             quantise_weights(steps - 1)
-            multiply(steps - 2)
 
             stats, row_moments = new_statistics()
-            quantise_stream(steps)
-            regroup(steps + 1)
-            quantise_stream(steps + 1)
             for j in range(PACK):
-                transpose_last(j)
-                quantise_last(j)
-            for j in range(PACK):
-                multiply_tile(steps - 1, j)
-                multiply_last(j)
+                for n in range(steps - LAG, steps):
+                    multiply_tile(n, j)
                 add_row_stats(nc, stats, sums[j], j)
                 add_bias(j, 3)
             half_row_moments(nc, row_moments, stats, vectors[:, 3, :])

from contextlib import ExitStack

import concourse.mybir as mybir
from concourse.masks import make_identity

BF16 = mybir.dt.bfloat16
F32 = mybir.dt.float32
U32 = mybir.dt.uint32
U8 = mybir.dt.uint8
FP8X4 = mybir.dt.float8_e4m3fn_x4
ACT = mybir.ActivationFunctionType
ALU = mybir.AluOpType
AX = mybir.AxisListType

P = 128
PACK = 4
K_PASS = P * PACK
BATCH = 8
TIMES = 64
COLS = BATCH * TIMES
CHANNELS = 512
K_CAT = 16384
PASSES = K_CAT // K_PASS
FM_PASS = 3
GROUP_ROWS = 16 * 2
EPS = 1e-5

CHUNK_PASSES = 4
VECTOR_TIMES = 44
LAG = 2
GROUP_NORM_STEP = 5
CHUNK_ORDER = (1, 2, 3, 4, 5, 0, 6, 7)

FLOPS = 2 * COLS * CHANNELS * (CHANNELS + K_CAT)


def load_stream_pass(nc, raw, stream, first_channel):
    channels = stream[:, first_channel : first_channel + K_PASS, :]
    nc.sync.dma_start(
        out=raw[:].rearrange("p b i t -> p b (i t)"),
        in_=channels.rearrange("b (p i) t -> p b (i t)", i=PACK),
    )


def group_on_vector(nc, grouped, raw):
    blocks = VECTOR_TIMES // 4
    nc.vector.tensor_copy(
        out=grouped[:].rearrange("p (b c r i) -> p b c i r", b=BATCH, r=4, i=PACK)[:, :, 0:blocks, :, :],
        in_=raw[:].rearrange("p b i (c r) -> p b c i r", r=4)[:, :, 0:blocks, :, :],
    )


def group_on_scalar(nc, grouped, raw):
    nc.scalar.copy(
        out=grouped[:].rearrange("p (b t i) -> p b t i", b=BATCH, i=PACK)[:, :, VECTOR_TIMES:TIMES, :],
        in_=raw[:].rearrange("p b i t -> p b t i")[:, :, VECTOR_TIMES:TIMES, :],
    )


def transpose_weights(nc, psum, grouped, words, first_word, ident):
    grouped_words = grouped[:].bitcast(F32).rearrange("q (c u) -> q c u", u=2)
    for half in range(2):
        planes = psum.tile([P, 2, 2 * P], F32, tag="bank", name="planes")
        for u in range(2):
            for i in range(2):
                columns = slice(first_word + u, first_word + 2 * P, 2)
                nc.tensor.transpose(
                    planes[:, u, i * P : (i + 1) * P], words[:, 2 * half + i, columns], ident[:]
                )
        nc.scalar.copy(
            out=grouped_words[:, half * 2 * P : (half + 1) * 2 * P, :],
            in_=planes[:].rearrange("q u c -> q c u"),
        )

def quantise(nc, pool, grouped, name):
    codes = pool.tile([P, COLS], U32, align_bytes=64, name=name + "_codes")
    scales = pool.tile([P, COLS], U8, align_bytes=64, name=name + "_scales")
    nc.vector.quantize_mx(out=codes[:].bitcast(FP8X4), scales=scales[:], in_=grouped[:])
    return codes, scales


def multiply_pass(nc, sums, weights, stream, start, stop):
    w_codes, w_scales = weights
    s_codes, s_scales = stream
    for j in range(PACK):
        rows = slice(j * P, (j + 1) * P)
        nc.tensor.matmul_mx(
            out=sums[j][:],
            lhsT=w_codes[:, rows].bitcast(FP8X4),
            lhsT_scale=w_scales[:, rows],
            rhs=s_codes[:].bitcast(FP8X4),
            rhs_scale=s_scales[:],
            start=start,
            stop=stop,
        )


def add_row_stats(nc, stats, source, j):
    for b in range(BATCH):
        nc.vector.bn_stats(
            out=stats[:, j, b, :, :].rearrange("p e s -> p (e s)"), in_=source[:, b * TIMES : (b + 1) * TIMES]
        )


def half_row_moments(nc, row_moments, stats, bias):
    mean = row_moments[:, 0, :, :, :].rearrange("p j b e -> p j (b e)")
    mean_of_squares = row_moments[:, 1, :, :, :].rearrange("p j b e -> p j (b e)")
    nc.vector.tensor_tensor(
        out=mean,
        in0=stats[:, :, :, :, 1].rearrange("p j b e -> p j (b e)"),
        in1=bias.unsqueeze(2).to_broadcast([P, PACK, 2 * BATCH]),
        op=ALU.add,
    )
    nc.vector.tensor_tensor(out=mean_of_squares, in0=mean, in1=mean, op=ALU.mult)
    nc.vector.scalar_tensor_tensor(
        out=mean_of_squares,
        in0=stats[:, :, :, :, 2].rearrange("p j b e -> p j (b e)"),
        scalar=2.0 / TIMES,
        in1=mean_of_squares,
        op0=ALU.mult,
        op1=ALU.add,
    )


def add_groups(nc, psum, row_moments, group_mean):
    sums = psum.tile([P, 2, PACK, BATCH, 2], F32, tag="bank", name="moment_sums")
    nc.tensor.matmul(
        out=sums[:].rearrange("p s j b e -> p (s j b e)"),
        lhsT=group_mean[:].rearrange("p g r -> p (g r)"),
        rhs=row_moments[:].rearrange("p s j b e -> p (s j b e)"),
        start=True,
        stop=True,
    )
    return sums


def group_moments(nc, work, sums):
    moments = work.tile([P, 2, BATCH], F32, name="moments")
    nc.vector.tensor_reduce(
        out=moments[:], in_=sums[:].rearrange("p s j b e -> p s b j e"), axis=AX.XY, op=ALU.add
    )
    var = work.tile([P, BATCH], F32, name="var")
    nc.vector.tensor_tensor(out=var[:], in0=moments[:, 0, :], in1=moments[:, 0, :], op=ALU.mult)
    nc.vector.tensor_tensor(out=var[:], in0=moments[:, 1, :], in1=var[:], op=ALU.subtract)
    nc.vector.tensor_scalar(out=var[:], in0=var[:], scalar1=0.0, scalar2=EPS, op0=ALU.max, op1=ALU.add)
    return moments, var


def square_root(nc, work, var):
    std = work.tile([P, BATCH], F32, name="std")
    nc.scalar.activation(out=std[:], in_=var[:], func=ACT.Sqrt)
    return std


def reciprocal(nc, work, std):
    rstd = work.tile([P, BATCH], F32, name="rstd")
    nc.vector.reciprocal(out=rstd[:], in_=std[:])
    return rstd


def normalise(nc, y, moments, rstd, batches):
    for b in batches:
        nc.vector.tensor_scalar(
            out=y[:, :, b, :],
            in0=y[:, :, b, :],
            scalar1=moments[:, 0, b : b + 1],
            scalar2=rstd[:, b : b + 1],
            op0=ALU.subtract,
            op1=ALU.mult,
        )


def affine_relu(nc, y, gamma, beta, result, tiles, batches):
    for j in tiles:
        nc.scalar.activation(
            out=result[:, batches, j, :],
            in_=y[:, j, batches, :],
            func=ACT.Relu,
            bias=beta[:, j : j + 1],
            scale=gamma[:, j : j + 1],
        )


def affine_on_vector(nc, y, gamma, beta, j, batches):
    nc.vector.tensor_scalar(
        out=y[:, j, batches, :],
        in0=y[:, j, batches, :],
        scalar1=gamma[:, j : j + 1],
        scalar2=beta[:, j : j + 1],
        op0=ALU.mult,
        op1=ALU.add,
    )


def relu_on_vector(nc, y, result, j, batches):
    nc.vector.tensor_scalar(
        out=result[:, batches, j, :], in0=y[:, j, batches, :], scalar1=0.0, scalar2=None, op0=ALU.max
    )


def tile_coarsepyramid_pc_k_kernel(
    tc,
    feature,
    prop_roi,
    prop_feature,
    conf_result_feature,
    w_cur,
    b_cur,
    g_cur,
    be_cur,
    w_prop,
    b_prop,
    g_prop,
    be_prop,
    out,
):
    nc = tc.nc

    def given_stream(g):
        if g == 0:
            return prop_roi, 0
        if g < FM_PASS:
            return prop_feature, (g - 1) * K_PASS
        return conf_result_feature, (g - FM_PASS - 1) * K_PASS

    with ExitStack() as stack:
        const = stack.enter_context(tc.tile_pool(name="const", bufs=1))
        work = stack.enter_context(tc.tile_pool(name="work", bufs=1))
        w_pool = stack.enter_context(tc.tile_pool(name="w_pool", bufs=3))
        raw_pool = stack.enter_context(tc.tile_pool(name="raw_pool", bufs=12))
        grouped_pool = stack.enter_context(tc.tile_pool(name="grouped_pool", bufs=4))
        operand_pool = stack.enter_context(tc.tile_pool(name="operand_pool", bufs=6))
        sums_pool = stack.enter_context(tc.psum_pool(name="sums_pool", bufs=1))
        bank_pool = stack.enter_context(tc.psum_pool(name="bank_pool", bufs=4))

        vectors_bf16 = const.tile([P, 6, 16], BF16)
        for v, vector in enumerate((b_cur, g_cur, be_cur, b_prop, g_prop, be_prop)):
            nc.scalar.dma_start(
                out=vectors_bf16[:, v, 0:PACK], in_=vector.rearrange("(p j) -> p j", j=PACK)
            )
        vectors = const.tile([P, 6, PACK], F32)

        one = const.tile([P, 1], F32)
        nc.vector.memset(one[:], 1.0)
        nc.scalar.activation(out=one[:], in_=one[:], func=ACT.Sqrt)
        no_bias = const.tile([P, PACK], F32)
        nc.vector.memset(no_bias[:], 0.0)
        ident = const.tile([P, P], F32)
        make_identity(nc, ident[:])
        same_group = const.tile([P, P // PACK], F32)
        nc.vector.tensor_reduce(
            out=same_group[:], in_=ident[:].rearrange("p (g r) -> p g r", r=PACK), axis=AX.X, op=ALU.add
        )
        group_mean = const.tile([P, P // PACK, PACK], F32)
        nc.vector.tensor_scalar(
            out=group_mean[:],
            in0=same_group[:].unsqueeze(2).to_broadcast([P, P // PACK, PACK]),
            scalar1=1.0 / GROUP_ROWS,
            scalar2=None,
            op0=ALU.mult,
        )

        Y_PASS = -1
        order = [Y_PASS] + [
            chunk * CHUNK_PASSES + c for chunk in CHUNK_ORDER for c in range(CHUNK_PASSES)
        ]
        steps = len(order)
        w_words = {}
        raws = {}
        w_cur_raw = const.tile([P, PACK, K_PASS], BF16)
        fm_raw = const.tile([P, BATCH, PACK, TIMES], BF16)

        def load_weights(first, count):
            passes = order[first : first + count]
            k0 = passes[0] * K_PASS
            pool = w_pool
            w_raw = pool.tile([P, PACK, count * K_PASS], BF16, name="w_raw%d" % count)
            nc.sync.dma_start(
                out=w_raw[:],
                in_=w_prop[:, k0 : k0 + count * K_PASS].rearrange("(p j) k -> p j k", j=PACK),
            )
            words = w_raw[:].bitcast(F32)
            for n, g in enumerate(passes):
                w_words[g] = (words, n * K_PASS // 2)


        def load(n):
            if n >= len(order):
                return
            g = order[n]
            if n == 0:
                nc.sync.dma_start(out=w_cur_raw[:], in_=w_cur.rearrange("(p j) k -> p j k", j=PACK))
                w_words[g] = (w_cur_raw[:].bitcast(F32), 0)
            if n % 4 == 1:
                load_weights(n, 4)
            if g == FM_PASS:
                raws[g] = fm_raw
            else:
                raw = raw_pool.tile([P, BATCH, PACK, TIMES], BF16, name="raw")
                source, first_channel = (feature, 0) if n == 0 else given_stream(g)
                load_stream_pass(nc, raw, source, first_channel)
                raws[g] = raw

        s_grouped = {}
        w_grouped = {}
        stream_operands = {}
        weight_operands = {}

        def regroup(n):
            if n < len(order):
                g = order[n]
                grouped = grouped_pool.tile([P, COLS * PACK], BF16, align_bytes=64, name="s_grouped")
                group_on_vector(nc, grouped, raws[g])
                group_on_scalar(nc, grouped, raws[g])
                s_grouped[g] = grouped

        def quantise_stream(n):
            if n < len(order):
                g = order[n]
                stream_operands[g] = quantise(nc, operand_pool, s_grouped[g], "s")

        def transpose_pass(n):
            g = order[n]
            grouped = grouped_pool.tile([P, CHANNELS * PACK], BF16, align_bytes=64, name="w_grouped")
            words, first_word = w_words[g]
            transpose_weights(nc, bank_pool, grouped, words, first_word, ident)
            w_grouped[g] = grouped

        def quantise_weights(n):
            g = order[n]
            weight_operands[g] = quantise(nc, operand_pool, w_grouped[g], "w")

        def multiply(n):
            g = order[n]
            multiply_pass(nc, sums, weight_operands[g], stream_operands[g], n <= 1, n == 0)

        def multiply_tile(n, j):
            w_codes, w_scales = weight_operands[order[n]]
            s_codes, s_scales = stream_operands[order[n]]
            rows = slice(j * P, (j + 1) * P)
            nc.tensor.matmul_mx(
                out=sums[j][:],
                lhsT=w_codes[:, rows].bitcast(FP8X4),
                lhsT_scale=w_scales[:, rows],
                rhs=s_codes[:].bitcast(FP8X4),
                rhs_scale=s_scales[:],
                start=False,
                stop=(n == steps - 1),
            )

        def new_sums():
            return [sums_pool.tile([P, COLS], F32, name="sums%d" % j) for j in range(PACK)]

        y = work.tile([P, PACK, BATCH, TIMES], F32, name="y")

        def new_statistics():
            stats = work.tile([P, PACK, BATCH, 2, 3], F32, name="stats")
            row_moments = work.tile([P, 2, PACK, BATCH, 2], F32, name="row_moments")
            return stats, row_moments

        def flat(tile, j):
            return tile[:, j, :, :].rearrange("p b t -> p (b t)")

        def add_bias(j, vector):
            nc.scalar.activation(
                out=flat(y, j), in_=sums[j][:], func=ACT.Identity, bias=vectors[:, vector, j : j + 1]
            )

        every_b = slice(0, BATCH)
        PREFETCH = 9
        for n in range(PREFETCH):
            load(n)
        with tc.manual_schedule():
            sums = new_sums()
            stats, row_moments = new_statistics()
            regroup(0)
            for n in range(steps):
                load(n + PREFETCH)
                transpose_pass(n)
                if n >= 1:
                    quantise_weights(n - 1)
                if n >= LAG:
                    multiply(n - LAG)
                if n == LAG:
                    nc.vector.tensor_copy(out=vectors[:], in_=vectors_bf16[:, :, 0:PACK])
                    for j in range(PACK):
                        if j < 2:
                            add_bias(j, 0)
                        else:
                            nc.vector.tensor_scalar(
                                out=flat(y, j), in0=sums[j][:], scalar1=vectors[:, 0, j : j + 1], scalar2=None, op0=ALU.add
                            )
                    sums = new_sums()
                quantise_stream(n)
                regroup(n + 1)
                g = n - GROUP_NORM_STEP
                if 0 <= g < PACK:
                    add_row_stats(nc, stats, flat(y, g), g)
                if g == 4:
                    half_row_moments(nc, row_moments, stats, no_bias[:])
                if g == 5:
                    moment_sums = add_groups(nc, bank_pool, row_moments, group_mean)
                if g == 6:
                    moments, var = group_moments(nc, work, moment_sums)
                if g == 7:
                    std = square_root(nc, work, var)
                if g == 8:
                    rstd = reciprocal(nc, work, std)
                if g in (8, 9):
                    normalise(nc, y, moments, rstd, range(4 * g - 32, 4 * g - 28))
                if 10 <= g < 10 + PACK:
                    affine_relu(nc, y, vectors[:, 1, :], vectors[:, 2, :], fm_raw, (g - 10,), every_b)
            quantise_weights(steps - 1)

            stats, row_moments = new_statistics()
            for j in range(PACK):
                for n in range(steps - LAG, steps):
                    multiply_tile(n, j)
                add_row_stats(nc, stats, sums[j], j)
                add_bias(j, 3)
            half_row_moments(nc, row_moments, stats, vectors[:, 3, :])
            moment_sums = add_groups(nc, bank_pool, row_moments, group_mean)
            moments, var = group_moments(nc, work, moment_sums)
            std = square_root(nc, work, var)
            rstd = reciprocal(nc, work, std)
            result = work.tile([P, BATCH, PACK, TIMES], F32, name="result")
            gamma, beta = vectors[:, 4, :], vectors[:, 5, :]
            pieces = [slice(0, 4), slice(4, 6), slice(6, 8)]
            for q in range(len(pieces) + 2):
                if q < len(pieces):
                    normalise(nc, y, moments, rstd, range(pieces[q].start, pieces[q].stop))
                    affine_relu(nc, y, gamma, beta, result, range(PACK - 1), pieces[q])
                if 1 <= q <= len(pieces):
                    affine_on_vector(nc, y, gamma, beta, PACK - 1, pieces[q - 1])
                if q >= 2:
                    batches = pieces[q - 2]
                    relu_on_vector(nc, y, result, PACK - 1, batches)
                    nc.sync.dma_start(
                        out=out[batches, :, :].rearrange("b (p j) t -> p b (j t)", j=PACK),
                        in_=result[:, batches, :, :].rearrange("p b j t -> p b (j t)"),
                    )
